import numpy as np
import ml_dtypes


def mxq(x, axis, fmt="e4m3"):
    dtype, down = {"e4m3": (ml_dtypes.float8_e4m3fn, 7), "e5m2": (ml_dtypes.float8_e5m2, 14)}[fmt]
    v = np.moveaxis(np.asarray(x, np.float32).astype(ml_dtypes.bfloat16).astype(np.float64), axis, -1)
    blocks = v.reshape(v.shape[:-1] + (-1, 32))
    amax = np.abs(blocks).max(-1, keepdims=True)
    byte = np.maximum(np.where(amax > 0, np.frexp(amax)[1] - 1 + 127, 0) - down, 1)
    scale = np.exp2(byte - 127.0)
    codes = (blocks / scale).astype(np.float32).astype(dtype).astype(np.float64)
    return np.moveaxis((codes * scale).reshape(v.shape), -1, axis)


WIDE = False


def mx_kscale(k):
    if not WIDE:
        return np.ones(k)
    levels = np.array([18, -18])
    if k % 512:
        return np.exp2(np.random.permutation(np.resize(levels, k // 32))).repeat(32)
    a = np.empty((k // 512, 16))
    for p in range(k // 512):
        a[p, :8] = np.random.permutation(np.resize(levels, 8))
        for g in range(8):
            far = levels[np.abs(levels - a[p, g]) >= 10]
            a[p, g + 8] = far[np.random.randint(len(far))]
    return np.exp2(a.ravel()).repeat(32)


BF16 = ml_dtypes.bfloat16


def bf(x):
    return np.asarray(x, np.float32).astype(BF16)


def f64(x):
    return np.asarray(x).astype(np.float64)


B, S, D, E, WINDOW = 2, 512, 1024, 1024, 10
HALF = WINDOW // 2
T = B * S


def window_softmax(scores):
    i = np.arange(S)[:, None]
    j = np.arange(S)[None, :]
    mask = np.abs(i - j) <= HALF
    scores = np.where(mask[None, :, :], scores, -1e9)
    e = np.exp(scores - scores.max(-1, keepdims=True))
    return e / e.sum(-1, keepdims=True)


def setup_inputs():
    u = mx_kscale(S)
    v = mx_kscale(E)
    s = mx_kscale(T)
    r = np.array([u[max(0, i - HALF):i + HALF + 1].min() for i in range(S)])
    x0 = bf(np.random.standard_normal((B, S, D)))
    Wq0 = bf(np.random.standard_normal((E, D)) / np.sqrt(D))
    bq = bf(np.random.standard_normal(E) * 0.1)
    k0 = bf(np.random.standard_normal((B, S, E)))
    rows = np.exp2(np.random.randint(-6, 1, (B, S, 1))) * 256.0
    g = bf(np.random.standard_normal((B, S, S)) * rows * r[None, :, None] / s.reshape(B, S, 1))
    q0 = f64(x0) @ f64(Wq0).T + f64(bq)
    p = window_softmax(q0 @ f64(k0).transpose(0, 2, 1) / np.sqrt(E))
    return {"x": bf(f64(x0) * s.reshape(B, S, 1)),
            "Wq": bf(f64(Wq0) / v[:, None]),
            "bq": bq,
            "k": bf(f64(k0) * v[None, None, :] / u[None, :, None]),
            "p": np.asarray(p, np.float32),
            "grad_out": g}


def reference(x, Wq, bq, k, p, grad_out):
    pf = f64(p)
    g = f64(grad_out)
    dz2 = pf * (g - (pf * g).sum(-1, keepdims=True))
    dh = mxq(dz2, 2, "e5m2") @ mxq(f64(k), 1, "e4m3")
    dq = (dh / np.sqrt(E)).reshape(T, E)
    dx = (mxq(dq, 1, "e5m2") @ mxq(f64(Wq), 0, "e4m3")).reshape(B, S, D)
    dWq = mxq(dq, 0, "e5m2").T @ mxq(f64(x).reshape(T, D), 0, "e4m3")
    return dx, dWq

@@ -1,0 +1,266 @@
+from contextlib import ExitStack
+
+import concourse.mybir as mybir
+from concourse.masks import make_identity
+
+B, S, D, E = 2, 512, 1024, 1024
+HALF = 5
+T = B * S
+P = 128
+WIN = 144
+WIN_START = (0, 120, 248, 368)
+
+F32 = mybir.dt.float32
+BF16 = mybir.dt.bfloat16
+U32 = mybir.dt.uint32
+U8 = mybir.dt.uint8
+E4M3 = mybir.dt.float8_e4m3fn_x4
+E5M2 = mybir.dt.float8_e5m2_x4
+MULT = mybir.AluOpType.mult
+SUB = mybir.AluOpType.subtract
+COPY = mybir.ActivationFunctionType.Copy
+
+FLOPS = 2 * B * S * S * E + 4 * T * E * D
+BAND = B * (S * (2 * HALF + 1) - HALF * (HALF + 1))
+BYTES = 2 * (T * D + E * D + T * E) + 6 * BAND + 4 * (T * D + E * D)
+
+
+def tile_localattention_pa_v_kernel(tc, x, Wq, bq, k, p, grad_out, out_0, out_1):
+    nc = tc.nc
+    with ExitStack() as ctx:
+        keep = ctx.enter_context(tc.tile_pool(name="keep", bufs=1))
+        outs = ctx.enter_context(tc.tile_pool(name="outs", bufs=16))
+        psum = ctx.enter_context(tc.psum_pool(name="psum", bufs=8))
+        ctx.enter_context(tc.manual_schedule())
+
+        def tiles(name, shape, dtype, n=2):
+            return [keep.tile(shape, dtype, name=f"{name}{i}", tag=f"{name}{i}", align_bytes=64) for i in range(n)]
+
+        ident = keep.tile([P, P], F32, name="ident", tag="ident", align_bytes=64)
+        pw = tiles("pw", [P, 4, WIN], F32)
+        gw = tiles("gw", [P, 4, WIN], BF16)
+        prod = keep.tile([P, 4, WIN], F32, name="prod", tag="prod", align_bytes=64)
+        rsum = tiles("rsum", [P, 4], F32)
+        dz = tiles("dz", [P, 4, S], BF16)
+        dzg = tiles("dzg", [P, S, 4], BF16)
+        dzc = tiles("dzc", [P, S], U32)
+        dzs = tiles("dzs", [P, S], U8)
+        raw, code, scale, grp = {}, {}, {}, {}
+        for n in ("k", "w", "x"):
+            raw[n] = tiles(n + "raw", [P, 4, 1024], BF16)
+        for n in ("k", "w", "x", "b"):
+            code[n] = tiles(n + "code", [P, 1024], U32)
+            scale[n] = tiles(n + "scale", [P, 1024], U8)
+        dqn = tiles("dqn", [P, 4, E], BF16)
+        raw["b"] = dqn
+        dqc = tiles("dqc", [P, 1024], U32)
+        dqs = tiles("dqs", [P, 1024], U8)
+
+        def grouped(n, b):
+            if (n, b) not in grp:
+                grp[n, b] = keep.tile([P, 4096], BF16, name=f"grp_{n}{b}", tag="grp", bufs=6, align_bytes=64)
+            return grp[n, b]
+
+        def bank():
+            return psum.tile([P, 512], F32, name="bank", tag="bank")
+
+        def load_window(b):
+            for dst, src in ((gw[b], grad_out[b]), (pw[b], p[b])):
+                for i in (0, 3):
+                    nc.sync.dma_start(out=dst[:, i, :], in_=src[P * i : P * (i + 1), WIN_START[i] : WIN_START[i] + WIN])
+                first = P * S + WIN_START[1]
+                step = P * S + P
+                both = src.rearrange("s j -> (s j)")[first : first + 2 * step].rearrange("(i y) -> i y", i=2)[:, : P * S]
+                nc.sync.dma_start(out=dst[:, 1:3, :], in_=both.rearrange("i (r j) -> r i j", j=S)[:, :, :WIN])
+
+        def load(n, b):
+            src = {"k": lambda: k[b], "x": lambda: x[b], "w": lambda: Wq[512 * b : 512 * (b + 1), :]}[n]()
+            nc.sync.dma_start(out=raw[n][b][:], in_=src.rearrange("(p j) c -> p j c", j=4))
+
+        def softmax_back(b):
+            for i in range(4):
+                nc.vector.scalar_tensor_tensor(out=prod[:, i, :], in0=gw[b][:, i, :], scalar=1.0, in1=pw[b][:, i, :], op0=MULT, op1=MULT, accum_out=rsum[b][:, i : i + 1])
+            for i in range(4):
+                cols = slice(WIN_START[i], WIN_START[i] + WIN)
+                nc.vector.scalar_tensor_tensor(out=dz[b][:, i, cols], in0=gw[b][:, i, :], scalar=rsum[b][:, i : i + 1], in1=pw[b][:, i, :], op0=SUB, op1=MULT)
+
+        def turn_dz(b):
+            banks = []
+            for h in range(2):
+                t = bank()
+                for i in range(2):
+                    words = dz[b][:, 2 * h + i, :].bitcast(F32)
+                    for u in range(2):
+                        at = 256 * u + 128 * i
+                        nc.tensor.transpose(t[:, at : at + 128], words[:, u : S // 2 : 2], ident[:])
+                banks.append(t)
+            return banks
+
+        def take_dz(b, banks, copies):
+            words = dzg[b][:].rearrange("p c j -> p (c j)").bitcast(F32).rearrange("p (t m u) -> p t m u", t=4, u=2)
+            for h in range(2):
+                copies[h](out=words[:, :, 64 * h : 64 * (h + 1), :], in_=banks[h][:].rearrange("p (u m t) -> p t m u", u=2, t=4))
+
+        def quant_dz(b):
+            nc.vector.quantize_mx(out=dzc[b][:].bitcast(E5M2), scales=dzs[b][:], in_=dzg[b][:].rearrange("p c j -> p (c j)"))
+
+        def group(n, b, copy, c0, c1):
+            copy(
+                out=grouped(n, b)[:].rearrange("p (c t) -> p c t", t=4)[:, c0:c1, :].rearrange("p (c i) t -> p c t i", i=4),
+                in_=raw[n][b][:, :, c0:c1].rearrange("p t (c i) -> p c t i", i=4),
+            )
+
+        def quant(n, b, c0, c1):
+            fmt = E5M2 if n == "b" else E4M3
+            nc.vector.quantize_mx(
+                out=code[n][b][:, c0:c1].bitcast(fmt), scales=scale[n][b][:, c0:c1], in_=grouped(n, b)[:, 4 * c0 : 4 * c1]
+            )
+
+        def dh(b, t, h):
+            o = bank()
+            cols = slice(512 * h, 512 * (h + 1))
+            nc.tensor.matmul_mx(
+                out=o[:], lhsT=dzc[b][:, P * t : P * (t + 1)].bitcast(E5M2), lhsT_scale=dzs[b][:, P * t : P * (t + 1)],
+                rhs=code["k"][b][:, cols].bitcast(E4M3), rhs_scale=scale["k"][b][:, cols], start=True, stop=True)
+            return o
+
+        def take_dq(b, t, h, o, eng):
+            dst = dqn[b][:, t, 512 * h : 512 * (h + 1)]
+            if eng == "A":
+                nc.scalar.activation(out=dst, in_=o[:], func=COPY, scale=1.0 / 32.0)
+            else:
+                nc.vector.tensor_scalar(out=dst, in0=o[:], scalar1=1.0 / 32.0, scalar2=None, op0=MULT)
+
+        def turn_dq(b, t):
+            o = bank()
+            words = dqn[b][:, t, :].bitcast(F32)
+            for g in range(2):
+                for u in range(2):
+                    at = 256 * g + 128 * u
+                    nc.tensor.transpose(o[:, at : at + 128], words[:, 256 * g + u : 256 * (g + 1) : 2], ident[:])
+            return o
+
+        def take_turned(b, t, o, copy):
+            copy(
+                out=grouped("a", b)[:, 1024 * t : 1024 * (t + 1)].bitcast(F32).rearrange("p (g m u) -> p g m u", g=2, u=2),
+                in_=o[:].rearrange("p (g u m) -> p g m u", g=2, u=2))
+
+        def quant_dq(b, t0, t1):
+            c = slice(256 * t0, 256 * t1)
+            nc.vector.quantize_mx(out=dqc[b][:, c].bitcast(E5M2), scales=dqs[b][:, c], in_=grouped("a", b)[:, 1024 * t0 : 1024 * t1])
+
+        def product(lhs, rhs, h):
+            o = bank()
+            cols = slice(512 * h, 512 * (h + 1))
+            for g in range(2):
+                lc, ls = lhs[g]
+                rc, rs = rhs[g]
+                nc.tensor.matmul_mx(out=o[:], lhsT=lc.bitcast(E5M2), lhsT_scale=ls, rhs=rc[:, cols].bitcast(E4M3), rhs_scale=rs[:, cols], start=(g == 0), stop=(g == 1))
+            return o
+
+        def out0(b, t, h, copy):
+            res = outs.tile([P, 512], F32, name="res", tag="res")
+            lhs = [(dqc[b][:, 256 * t + P * g : 256 * t + P * (g + 1)], dqs[b][:, 256 * t + P * g : 256 * t + P * (g + 1)]) for g in range(2)]
+            rhs = [(code["w"][g], scale["w"][g]) for g in range(2)]
+            o = product(lhs, rhs, h)
+            copy(out=res[:], in_=o[:])
+            nc.sync.dma_start(out=out_0[b].rearrange("(m t) d -> m t d", t=4)[:, t, 512 * h : 512 * (h + 1)], in_=res[:])
+
+        def out1(e, h, copy):
+            res = outs.tile([P, 512], F32, name="res", tag="res")
+            cols = slice(P * e, P * (e + 1))
+            lhs = [(code["b"][g][:, cols], scale["b"][g][:, cols]) for g in range(2)]
+            rhs = [(code["x"][g], scale["x"][g]) for g in range(2)]
+            o = product(lhs, rhs, h)
+            copy(out=res[:], in_=o[:])
+            nc.sync.dma_start(out=out_1[cols, 512 * h : 512 * (h + 1)], in_=res[:])
+
+        V, A = nc.vector.tensor_copy, nc.scalar.copy
+
+        make_identity(nc, ident[:])
+        for b in range(2):
+            nc.vector.memset(dz[b][:], 0.0)
+        load_window(0)
+        load("k", 0)
+        load_window(1)
+        load("k", 1)
+        load("w", 0)
+        load("w", 1)
+        load("x", 0)
+        load("x", 1)
+
+        def il(n, b, cs, copy):
+            for c in cs:
+                group(n, b, copy, 256 * c, 256 * (c + 1))
+
+        def qh(n, b, h):
+            quant(n, b, 512 * h, 512 * (h + 1))
+
+        def q(n, b, c0, c1):
+            quant(n, b, 256 * c0, 256 * c1)
+
+        softmax_back(0)
+        banks = turn_dz(0)
+        il("k", 0, (0, 1), V)
+        take_dz(0, banks, (A, A))
+        il("k", 0, (3, 2), A)
+        q("k", 0, 0, 2)
+        quant_dz(0)
+        softmax_back(1)
+        q("k", 0, 2, 4)
+        for h in range(2):
+            for t in range(4):
+                take_dq(0, t, h, dh(0, t, h), "A")
+        il("k", 1, (0, 1, 2, 3), V)
+        take_dz(1, turn_dz(1), (V, V))
+        q("k", 1, 0, 2)
+        quant_dz(1)
+        q("k", 1, 2, 4)
+        for t in range(4):
+            take_turned(0, t, turn_dq(0, t), A)
+        il("w", 0, (0, 1), V)
+        il("w", 1, (0, 1), V)
+        q("w", 0, 0, 2)
+        quant_dq(0, 0, 2)
+        q("w", 1, 0, 2)
+        quant_dq(0, 2, 4)
+        for h in range(2):
+            for t in range(4):
+                take_dq(1, t, h, dh(1, t, h), "A")
+        for t in range(4):
+            out0(0, t, 0, A)
+        il("w", 0, (2, 3), V)
+        il("w", 1, (2, 3), V)
+        for t in range(4):
+            take_turned(1, t, turn_dq(1, t), A)
+        q("w", 0, 2, 4)
+        q("w", 1, 2, 4)
+        quant_dq(1, 0, 2)
+        quant_dq(1, 2, 4)
+        for t in range(4):
+            out0(0, t, 1, A)
+        il("x", 0, (0, 1, 2, 3), V)
+        il("x", 1, (0, 1), V)
+        for t in range(4):
+            out0(1, t, 0, A)
+        q("x", 0, 0, 2)
+        il("x", 1, (3,), A)
+        q("x", 1, 0, 2)
+        il("x", 1, (2,), V)
+        il("b", 0, (0,), V)
+        q("x", 0, 2, 4)
+        il("b", 1, (0,), V)
+        for t in range(4):
+            out0(1, t, 1, A)
+        q("b", 0, 0, 1)
+        q("b", 1, 0, 1)
+        q("x", 1, 2, 4)
+        for c in range(4):
+            if c < 3:
+                il("b", 0, (c + 1,), V)
+                il("b", 1, (c + 1,), V)
+                q("b", 0, c + 1, c + 2)
+                q("b", 1, c + 1, c + 2)
+            for h in range(2):
+                for e in (2 * c, 2 * c + 1):
+                    out1(e, h, V if c == 3 and e % 2 else A)

@@ -7,8 +7,9 @@ B, S, D, E = 2, 512, 1024, 1024
 HALF = 5
 T = B * S
 P = 128
-WIN = 144
-WIN_START = (0, 120, 248, 368)
+WIN = 152
+WIN_STEP = 120
+WIN_PITCH = 160
 
 F32 = mybir.dt.float32
 BF16 = mybir.dt.bfloat16
@@ -29,7 +30,7 @@ def tile_localattention_pa_v_kernel(tc, x, Wq, bq, k, p, grad_out, out_0, out_1)
     nc = tc.nc
     with ExitStack() as ctx:
         keep = ctx.enter_context(tc.tile_pool(name="keep", bufs=1))
-        outs = ctx.enter_context(tc.tile_pool(name="outs", bufs=16))
+        outs = ctx.enter_context(tc.tile_pool(name="outs", bufs=10))
         psum = ctx.enter_context(tc.psum_pool(name="psum", bufs=8))
         ctx.enter_context(tc.manual_schedule())
 
@@ -37,230 +38,273 @@ def tile_localattention_pa_v_kernel(tc, x, Wq, bq, k, p, grad_out, out_0, out_1)
             return [keep.tile(shape, dtype, name=f"{name}{i}", tag=f"{name}{i}", align_bytes=64) for i in range(n)]
 
         ident = keep.tile([P, P], F32, name="ident", tag="ident", align_bytes=64)
-        pw = tiles("pw", [P, 4, WIN], F32)
-        gw = tiles("gw", [P, 4, WIN], BF16)
-        prod = keep.tile([P, 4, WIN], F32, name="prod", tag="prod", align_bytes=64)
+        ident_bf = keep.tile([P, P], BF16, name="ident_bf", tag="ident_bf", align_bytes=64)
+        pw = tiles("pw", [P, 4, WIN_PITCH], F32)
+        gw = tiles("gw", [P, 4, WIN_PITCH], BF16)
+        prod = keep.tile([P, 4, WIN_PITCH], F32, name="prod", tag="prod", align_bytes=64)
         rsum = tiles("rsum", [P, 4], F32)
-        dz = tiles("dz", [P, 4, S], BF16)
-        dzg = tiles("dzg", [P, S, 4], BF16)
+        dz = [tiles(f"dz{b}_", [P, S], BF16, 4) for b in range(B)]
+        dzg = tiles("dzg", [P, 4 * S], BF16)
         dzc = tiles("dzc", [P, S], U32)
         dzs = tiles("dzs", [P, S], U8)
-        raw, code, scale, grp = {}, {}, {}, {}
-        for n in ("k", "w", "x"):
-            raw[n] = tiles(n + "raw", [P, 4, 1024], BF16)
-        for n in ("k", "w", "x", "b"):
-            code[n] = tiles(n + "code", [P, 1024], U32)
-            scale[n] = tiles(n + "scale", [P, 1024], U8)
-        dqn = tiles("dqn", [P, 4, E], BF16)
-        raw["b"] = dqn
-        dqc = tiles("dqc", [P, 1024], U32)
-        dqs = tiles("dqs", [P, 1024], U8)
+        raw = {}
+        code = {n: tiles(n + "code", [P, 1024], U32) for n in ("k", "w", "x")}
+        scale = {n: tiles(n + "scale", [P, 1024], U8) for n in ("k", "w", "x")}
+        dq = {n: tiles("dq" + n, [P, 1024], BF16, 8) for n in ("a", "b")}
+        dqc = {n: tiles("dqc" + n, [P, 256], U32, 8) for n in ("a", "b")}
+        dqs = {n: tiles("dqs" + n, [P, 256], U8, 8) for n in ("a", "b")}
+        grp, res = {}, {}
 
-        def grouped(n, b):
-            if (n, b) not in grp:
-                grp[n, b] = keep.tile([P, 4096], BF16, name=f"grp_{n}{b}", tag="grp", bufs=6, align_bytes=64)
-            return grp[n, b]
+        def grouped(n, b, h):
+            if (n, b, h) not in grp:
+                grp[n, b, h] = keep.tile([P, 2048], BF16, name=f"grp_{n}{b}{h}", tag="grp", bufs=6, align_bytes=64)
+            return grp[n, b, h]
 
-        def bank():
-            return psum.tile([P, 512], F32, name="bank", tag="bank")
+        def bank(dtype=F32, cols=512):
+            return psum.tile([P, cols], dtype, name="bank", tag="bank")
 
-        def load_window(b):
-            for dst, src in ((gw[b], grad_out[b]), (pw[b], p[b])):
-                for i in (0, 3):
-                    nc.sync.dma_start(out=dst[:, i, :], in_=src[P * i : P * (i + 1), WIN_START[i] : WIN_START[i] + WIN])
-                first = P * S + WIN_START[1]
-                step = P * S + P
-                both = src.rearrange("s j -> (s j)")[first : first + 2 * step].rearrange("(i y) -> i y", i=2)[:, : P * S]
-                nc.sync.dma_start(out=dst[:, 1:3, :], in_=both.rearrange("i (r j) -> r i j", j=S)[:, :, :WIN])
+        V, A = "V", "A"
+
+        def copy(eng, out, in_):
+            if eng == V:
+                nc.vector.tensor_copy(out=out, in_=in_)
+            else:
+                nc.scalar.copy(out=out, in_=in_)
+
+        def load_window(b, i0=0, i1=4):
+            step = P * S + WIN_STEP
+            for dst, src in ((gw[b], grad_out), (pw[b], p)):
+                flat = src.rearrange("b s j -> (b s j)")
+                if b == 0:
+                    rows = flat[: 4 * step].rearrange("(i y) -> i y", i=4)[:, : P * S]
+                    win = rows.rearrange("i (r j) -> r i j", j=S)[:, :, :WIN]
+                else:
+                    rows = flat[B * S * S - 4 * step :].rearrange("(i y) -> i y", i=4)[:, WIN_STEP:]
+                    win = rows.rearrange("i (r j) -> r i j", j=S)[:, :, S - WIN :]
+                nc.sync.dma_start(out=dst[:, i0:i1, :WIN], in_=win[:, i0:i1, :])
+
+        def rows_of(n, b):
+            return {"k": lambda: k[b], "x": lambda: x[b], "w": lambda: Wq[512 * b : 512 * (b + 1), :]}[n]().rearrange("(p j) c -> p j c", j=4)
 
         def load(n, b):
-            src = {"k": lambda: k[b], "x": lambda: x[b], "w": lambda: Wq[512 * b : 512 * (b + 1), :]}[n]()
-            nc.sync.dma_start(out=raw[n][b][:], in_=src.rearrange("(p j) c -> p j c", j=4))
-
-        def softmax_back(b):
-            for i in range(4):
-                nc.vector.scalar_tensor_tensor(out=prod[:, i, :], in0=gw[b][:, i, :], scalar=1.0, in1=pw[b][:, i, :], op0=MULT, op1=MULT, accum_out=rsum[b][:, i : i + 1])
-            for i in range(4):
-                cols = slice(WIN_START[i], WIN_START[i] + WIN)
-                nc.vector.scalar_tensor_tensor(out=dz[b][:, i, cols], in0=gw[b][:, i, :], scalar=rsum[b][:, i : i + 1], in1=pw[b][:, i, :], op0=SUB, op1=MULT)
-
-        def turn_dz(b):
-            banks = []
+            t = keep.tile([P, 4, 1024], BF16, name=f"raw_{n}{b}", tag=f"raw_{n}{b}", align_bytes=64)
+            nc.sync.dma_start(out=t[:], in_=rows_of(n, b))
             for h in range(2):
-                t = bank()
-                for i in range(2):
-                    words = dz[b][:, 2 * h + i, :].bitcast(F32)
-                    for u in range(2):
-                        at = 256 * u + 128 * i
-                        nc.tensor.transpose(t[:, at : at + 128], words[:, u : S // 2 : 2], ident[:])
-                banks.append(t)
-            return banks
+                raw[n, b, h] = t[:, :, 512 * h : 512 * (h + 1)]
 
-        def take_dz(b, banks, copies):
-            words = dzg[b][:].rearrange("p c j -> p (c j)").bitcast(F32).rearrange("p (t m u) -> p t m u", t=4, u=2)
-            for h in range(2):
-                copies[h](out=words[:, :, 64 * h : 64 * (h + 1), :], in_=banks[h][:].rearrange("p (u m t) -> p t m u", u=2, t=4))
+        def load_half(n, b, h):
+            t = keep.tile([P, 4, 512], BF16, name=f"raw_{n}{b}{h}", tag=f"raw_{n}{b}{h}", align_bytes=64)
+            nc.sync.dma_start(out=t[:], in_=rows_of(n, b)[:, :, 512 * h : 512 * (h + 1)])
+            raw[n, b, h] = t[:]
+
+        def band(i):
+            lo, hi = max(P * i - 8, 0), min(P * i + 136, S)
+            return slice(lo, hi), slice(lo - WIN_STEP * i, hi - WIN_STEP * i)
+
+        def row_sums(b, tiles_):
+            for i in tiles_:
+                w = band(i)[1]
+                nc.vector.scalar_tensor_tensor(out=prod[:, i, w], in0=gw[b][:, i, w], scalar=1.0, in1=pw[b][:, i, w], op0=MULT, op1=MULT, accum_out=rsum[b][:, i : i + 1])
+
+        def soft(b, tiles_):
+            for i in tiles_:
+                cols, w = band(i)
+                nc.vector.scalar_tensor_tensor(out=dz[b][i][:, cols], in0=gw[b][:, i, w], scalar=rsum[b][:, i : i + 1], in1=pw[b][:, i, w], op0=SUB, op1=MULT)
+
+        def turn_dz(b, h):
+            t = bank()
+            for i in range(2):
+                words = dz[b][2 * h + i][:].bitcast(F32)
+                for u in range(2):
+                    at = 256 * u + 128 * i
+                    nc.tensor.transpose(t[:, at : at + 128], words[:, u : S // 2 : 2], ident[:])
+            return t
+
+        def take_dz(b, h, t, eng):
+            words = dzg[b][:].bitcast(F32).rearrange("p (t m u) -> p t m u", t=4, u=2)
+            copy(eng, words[:, :, 64 * h : 64 * (h + 1), :], t[:].rearrange("p (u m t) -> p t m u", u=2, t=4))
 
         def quant_dz(b):
-            nc.vector.quantize_mx(out=dzc[b][:].bitcast(E5M2), scales=dzs[b][:], in_=dzg[b][:].rearrange("p c j -> p (c j)"))
+            nc.vector.quantize_mx(out=dzc[b][:].bitcast(E5M2), scales=dzs[b][:], in_=dzg[b][:])
 
-        def group(n, b, copy, c0, c1):
-            copy(
-                out=grouped(n, b)[:].rearrange("p (c t) -> p c t", t=4)[:, c0:c1, :].rearrange("p (c i) t -> p c t i", i=4),
-                in_=raw[n][b][:, :, c0:c1].rearrange("p t (c i) -> p c t i", i=4),
-            )
+        def weave_pe(n, b, h, a):
+            src = raw[n, b, h]
+            t = bank(BF16, 1024)
+            for c in range(2):
+                cols = slice(256 * a + P * c, 256 * a + P * (c + 1))
+                nc.tensor.matmul(t[:, 512 * c : 512 * (c + 1)], lhsT=ident_bf[:], rhs=src[:, :, cols].rearrange("p j c -> p c j"), start=True, stop=True)
+            return t
 
-        def quant(n, b, c0, c1):
-            fmt = E5M2 if n == "b" else E4M3
-            nc.vector.quantize_mx(
-                out=code[n][b][:, c0:c1].bitcast(fmt), scales=scale[n][b][:, c0:c1], in_=grouped(n, b)[:, 4 * c0 : 4 * c1]
-            )
+        def take_k(b, g, a, t, eng):
+            dst = grouped("k", b, g)[:].rearrange("p (t m j) -> p t m j", t=4, j=4)[:, :, 64 * a : 64 * (a + 1), :]
+            copy(eng, dst, t[:].rearrange("p (m t j) -> p t m j", t=4, j=4))
 
-        def dh(b, t, h):
-            o = bank()
+        def weave_k(b, g, a, eng):
+            src = raw["k", b, g]
+            dst = grouped("k", b, g)[:].rearrange("p (t m j) -> p t m j", t=4, j=4)[:, :, 64 * a : 64 * (a + 1), :]
+            copy(eng, dst.rearrange("p t (n i) j -> p n t i j", i=2), src[:, :, 256 * a : 256 * (a + 1)].rearrange("p j (n i t) -> p n t i j", i=2, t=4))
+
+        def weave(n, b, h, a, eng):
+            dst = grouped(n, b, h)[:, 1024 * a : 1024 * (a + 1)].rearrange("p (c i t) -> p c t i", i=4, t=4)
+            copy(eng, dst, raw[n, b, h][:, :, 256 * a : 256 * (a + 1)].rearrange("p t (c i) -> p c t i", i=4))
+
+        def take_woven(n, b, h, a, t, eng):
+            copy(eng, grouped(n, b, h)[:, 1024 * a : 1024 * (a + 1)], t[:])
+
+        def quant(n, b, h):
             cols = slice(512 * h, 512 * (h + 1))
-            nc.tensor.matmul_mx(
-                out=o[:], lhsT=dzc[b][:, P * t : P * (t + 1)].bitcast(E5M2), lhsT_scale=dzs[b][:, P * t : P * (t + 1)],
-                rhs=code["k"][b][:, cols].bitcast(E4M3), rhs_scale=scale["k"][b][:, cols], start=True, stop=True)
+            nc.vector.quantize_mx(out=code[n][b][:, cols].bitcast(E4M3), scales=scale[n][b][:, cols], in_=grouped(n, b, h)[:])
+
+        def kop(b, s):
+            cols = slice(P * s, P * (s + 1))
+            return code["k"][b][:, cols].bitcast(E4M3), scale["k"][b][:, cols]
+
+        def zop(b, t):
+            cols = slice(P * t, P * (t + 1))
+            return dzc[b][:, cols].bitcast(E5M2), dzs[b][:, cols]
+
+        def four(pairs):
+            o = bank()
+            for t, (still, moving) in enumerate(pairs):
+                nc.tensor.matmul_mx(out=o[:, P * t : P * (t + 1)], lhsT=still[0], lhsT_scale=still[1], rhs=moving[0], rhs_scale=moving[1], start=True, stop=True)
             return o
 
-        def take_dq(b, t, h, o, eng):
-            dst = dqn[b][:, t, 512 * h : 512 * (h + 1)]
-            if eng == "A":
-                nc.scalar.activation(out=dst, in_=o[:], func=COPY, scale=1.0 / 32.0)
+        def take_dq(dst, o, eng):
+            dst = dst.rearrange("p (c t) -> p c t", t=4)
+            src = o[:].rearrange("p (t c) -> p c t", t=4)
+            if eng == A:
+                nc.scalar.activation(out=dst, in_=src, func=COPY, scale=1.0 / 32.0)
             else:
-                nc.vector.tensor_scalar(out=dst, in0=o[:], scalar1=1.0 / 32.0, scalar2=None, op0=MULT)
+                nc.vector.tensor_scalar(out=dst, in0=src, scalar1=1.0 / 32.0, scalar2=None, op0=MULT)
 
-        def turn_dq(b, t):
-            o = bank()
-            words = dqn[b][:, t, :].bitcast(F32)
-            for g in range(2):
-                for u in range(2):
-                    at = 256 * g + 128 * u
-                    nc.tensor.transpose(o[:, at : at + 128], words[:, 256 * g + u : 256 * (g + 1) : 2], ident[:])
-            return o
+        def dqa(b, t, g, eng):
+            o = four([(kop(b, 4 * g + j), zop(b, t)) for j in range(4)])
+            take_dq(dq["a"][4 * b + t][:, 512 * g : 512 * (g + 1)], o, eng)
 
-        def take_turned(b, t, o, copy):
-            copy(
-                out=grouped("a", b)[:, 1024 * t : 1024 * (t + 1)].bitcast(F32).rearrange("p (g m u) -> p g m u", g=2, u=2),
-                in_=o[:].rearrange("p (g u m) -> p g m u", g=2, u=2))
+        def dqb(s, b, eng):
+            o = four([(zop(b, j), kop(b, s)) for j in range(4)])
+            take_dq(dq["b"][s][:, 512 * b : 512 * (b + 1)], o, eng)
 
-        def quant_dq(b, t0, t1):
-            c = slice(256 * t0, 256 * t1)
-            nc.vector.quantize_mx(out=dqc[b][:, c].bitcast(E5M2), scales=dqs[b][:, c], in_=grouped("a", b)[:, 1024 * t0 : 1024 * t1])
+        def quant_dq(n, i):
+            nc.vector.quantize_mx(out=dqc[n][i][:].bitcast(E5M2), scales=dqs[n][i][:], in_=dq[n][i][:])
 
-        def product(lhs, rhs, h):
+        def product(n, i, h, eng):
+            other = {"a": "w", "b": "x"}[n]
+            if (n, i) not in res:
+                res[n, i] = outs.tile([P, 1024], F32, name="res", tag="res")
             o = bank()
             cols = slice(512 * h, 512 * (h + 1))
             for g in range(2):
-                lc, ls = lhs[g]
-                rc, rs = rhs[g]
-                nc.tensor.matmul_mx(out=o[:], lhsT=lc.bitcast(E5M2), lhsT_scale=ls, rhs=rc[:, cols].bitcast(E4M3), rhs_scale=rs[:, cols], start=(g == 0), stop=(g == 1))
-            return o
+                mine = slice(P * g, P * (g + 1))
+                nc.tensor.matmul_mx(out=o[:], lhsT=dqc[n][i][:, mine].bitcast(E5M2), lhsT_scale=dqs[n][i][:, mine],
+                                    rhs=code[other][g][:, cols].bitcast(E4M3), rhs_scale=scale[other][g][:, cols], start=(g == 0), stop=(g == 1))
+            copy(eng, res[n, i][:, cols], o[:])
 
-        def out0(b, t, h, copy):
-            res = outs.tile([P, 512], F32, name="res", tag="res")
-            lhs = [(dqc[b][:, 256 * t + P * g : 256 * t + P * (g + 1)], dqs[b][:, 256 * t + P * g : 256 * t + P * (g + 1)]) for g in range(2)]
-            rhs = [(code["w"][g], scale["w"][g]) for g in range(2)]
-            o = product(lhs, rhs, h)
-            copy(out=res[:], in_=o[:])
-            nc.sync.dma_start(out=out_0[b].rearrange("(m t) d -> m t d", t=4)[:, t, 512 * h : 512 * (h + 1)], in_=res[:])
-
-        def out1(e, h, copy):
-            res = outs.tile([P, 512], F32, name="res", tag="res")
-            cols = slice(P * e, P * (e + 1))
-            lhs = [(code["b"][g][:, cols], scale["b"][g][:, cols]) for g in range(2)]
-            rhs = [(code["x"][g], scale["x"][g]) for g in range(2)]
-            o = product(lhs, rhs, h)
-            copy(out=res[:], in_=o[:])
-            nc.sync.dma_start(out=out_1[cols, 512 * h : 512 * (h + 1)], in_=res[:])
-
-        V, A = nc.vector.tensor_copy, nc.scalar.copy
+        def store(n, i, h=None):
+            cols = slice(0, 1024) if h is None else slice(512 * h, 512 * (h + 1))
+            g, t = divmod(i, 4)
+            dst = out_0[g] if n == "a" else out_1[512 * g : 512 * (g + 1), :]
+            nc.sync.dma_start(out=dst.rearrange("(m t) d -> m t d", t=4)[:, t, cols], in_=res[n, i][:, cols])
 
         make_identity(nc, ident[:])
-        for b in range(2):
-            nc.vector.memset(dz[b][:], 0.0)
+        make_identity(nc, ident_bf[:])
+        for b in range(B):
+            for i in range(4):
+                nc.vector.memset(dz[b][i][:], 0.0)
         load_window(0)
-        load("k", 0)
+        load_half("k", 0, 0)
+        load_half("k", 0, 1)
+        load_half("w", 0, 0)
+        load_half("w", 1, 0)
         load_window(1)
+        load_half("w", 0, 1)
+        load_half("w", 1, 1)
         load("k", 1)
-        load("w", 0)
-        load("w", 1)
         load("x", 0)
         load("x", 1)
-
-        def il(n, b, cs, copy):
-            for c in cs:
-                group(n, b, copy, 256 * c, 256 * (c + 1))
-
-        def qh(n, b, h):
-            quant(n, b, 512 * h, 512 * (h + 1))
-
-        def q(n, b, c0, c1):
-            quant(n, b, 256 * c0, 256 * c1)
-
-        softmax_back(0)
-        banks = turn_dz(0)
-        il("k", 0, (0, 1), V)
-        take_dz(0, banks, (A, A))
-        il("k", 0, (3, 2), A)
-        q("k", 0, 0, 2)
+        row_sums(0, range(4))
+        soft(0, range(4))
+        for h in range(2):
+            take_dz(0, h, turn_dz(0, h), A)
+        for a in range(2):
+            weave_k(0, 0, a, V)
+        for a in range(2):
+            take_k(0, 1, a, weave_pe("k", 0, 1, a), A)
+        quant("k", 0, 0)
         quant_dz(0)
-        softmax_back(1)
-        q("k", 0, 2, 4)
+        for t in range(4):
+            dqa(0, t, 0, A)
+        weave("w", 0, 0, 0, V)
+        weave("w", 0, 0, 1, V)
+        quant("k", 0, 1)
+        for t in range(4):
+            dqa(0, t, 1, A)
+        weave("w", 1, 0, 0, V)
+        weave("w", 1, 0, 1, V)
+        quant("w", 0, 0)
+        quant_dq("a", 0)
+        quant("w", 1, 0)
+        quant_dq("a", 1)
+        row_sums(1, range(4))
+        quant_dq("a", 2)
+        soft(1, range(4))
+        quant_dq("a", 3)
+        dqb(0, 0, A)
+        for t in range(4):
+            product("a", t, 0, A)
+            store("a", t, 0)
+            dqb(t + 1, 0, A)
         for h in range(2):
-            for t in range(4):
-                take_dq(0, t, h, dh(0, t, h), "A")
-        il("k", 1, (0, 1, 2, 3), V)
-        take_dz(1, turn_dz(1), (V, V))
-        q("k", 1, 0, 2)
+            take_dz(1, h, turn_dz(1, h), A)
+        for t in range(4):
+            weave("w", t // 2, 1, t % 2, V)
+        quant("w", 0, 1)
+        weave_k(1, 0, 0, V)
+        quant("w", 1, 1)
+        for s in range(5, 8):
+            dqb(s, 0, A)
+        for t in range(4):
+            product("a", t, 1, A)
+            store("a", t, 1)
+        weave_k(1, 0, 1, V)
         quant_dz(1)
-        q("k", 1, 2, 4)
+        quant("k", 1, 0)
         for t in range(4):
-            take_turned(0, t, turn_dq(0, t), A)
-        il("w", 0, (0, 1), V)
-        il("w", 1, (0, 1), V)
-        q("w", 0, 0, 2)
-        quant_dq(0, 0, 2)
-        q("w", 1, 0, 2)
-        quant_dq(0, 2, 4)
-        for h in range(2):
-            for t in range(4):
-                take_dq(1, t, h, dh(1, t, h), "A")
+            dqa(1, t, 0, A)
+        weave_k(1, 1, 0, V)
+        weave_k(1, 1, 1, V)
+        weave("x", 0, 0, 0, V)
+        quant("k", 1, 1)
         for t in range(4):
-            out0(0, t, 0, A)
-        il("w", 0, (2, 3), V)
-        il("w", 1, (2, 3), V)
+            dqa(1, t, 1, A)
+        weave("x", 0, 0, 1, V)
+        weave("x", 1, 0, 0, V)
+        quant_dq("a", 4)
+        weave("x", 1, 0, 1, V)
+        quant_dq("a", 5)
+        quant("x", 0, 0)
+        quant_dq("a", 6)
+        quant("x", 1, 0)
+        quant_dq("a", 7)
         for t in range(4):
-            take_turned(1, t, turn_dq(1, t), A)
-        q("w", 0, 2, 4)
-        q("w", 1, 2, 4)
-        quant_dq(1, 0, 2)
-        quant_dq(1, 2, 4)
-        for t in range(4):
-            out0(0, t, 1, A)
-        il("x", 0, (0, 1, 2, 3), V)
-        il("x", 1, (0, 1), V)
-        for t in range(4):
-            out0(1, t, 0, A)
-        q("x", 0, 0, 2)
-        il("x", 1, (3,), A)
-        q("x", 1, 0, 2)
-        il("x", 1, (2,), V)
-        il("b", 0, (0,), V)
-        q("x", 0, 2, 4)
-        il("b", 1, (0,), V)
-        for t in range(4):
-            out0(1, t, 1, A)
-        q("b", 0, 0, 1)
-        q("b", 1, 0, 1)
-        q("x", 1, 2, 4)
-        for c in range(4):
-            if c < 3:
-                il("b", 0, (c + 1,), V)
-                il("b", 1, (c + 1,), V)
-                q("b", 0, c + 1, c + 2)
-                q("b", 1, c + 1, c + 2)
+            dqb(t, 1, V)
             for h in range(2):
-                for e in (2 * c, 2 * c + 1):
-                    out1(e, h, V if c == 3 and e % 2 else A)
+                product("a", 4 + t, h, A)
+            store("a", 4 + t)
+            if t > 0:
+                quant_dq("b", t - 1)
+        dqb(4, 1, V)
+        quant_dq("b", 3)
+        for s in range(8):
+            if s < 3:
+                dqb(5 + s, 1, A)
+            if s < 4:
+                weave("x", s // 2, 1, s % 2, V)
+                quant_dq("b", 4 + s)
+            if s in (4, 5):
+                quant("x", s - 4, 1)
+            product("b", s, 0, A)
+            store("b", s, 0)
+        for s in range(8):
+            product("b", s, 1, (A, V)[s % 2])
+            store("b", s, 1)

@@ -10,6 +10,7 @@ P = 128
 WIN = 152
 WIN_STEP = 120
 WIN_PITCH = 160
+GRP_BUFS = 3
 
 F32 = mybir.dt.float32
 BF16 = mybir.dt.bfloat16
@@ -47,18 +48,17 @@ def tile_localattention_pa_v_kernel(tc, x, Wq, bq, k, p, grad_out, out_0, out_1)
         dzg = tiles("dzg", [P, 4 * S], BF16)
         dzc = tiles("dzc", [P, S], U32)
         dzs = tiles("dzs", [P, S], U8)
-        raw = {}
+        raw, grp, res = {}, {}, {}
         code = {n: tiles(n + "code", [P, 1024], U32) for n in ("k", "w", "x")}
         scale = {n: tiles(n + "scale", [P, 1024], U8) for n in ("k", "w", "x")}
-        dq = {n: tiles("dq" + n, [P, 1024], BF16, 8) for n in ("a", "b")}
-        dqc = {n: tiles("dqc" + n, [P, 256], U32, 8) for n in ("a", "b")}
-        dqs = {n: tiles("dqs" + n, [P, 256], U8, 8) for n in ("a", "b")}
-        grp, res = {}, {}
+        dq = {n: tiles("dq" + n, [P, 4096], BF16) for n in ("a", "b")}
+        dqc = {n: tiles("dqc" + n, [P, 1024], U32) for n in ("a", "b")}
+        dqs = {n: tiles("dqs" + n, [P, 1024], U8) for n in ("a", "b")}
 
-        def grouped(n, b, h):
-            if (n, b, h) not in grp:
-                grp[n, b, h] = keep.tile([P, 2048], BF16, name=f"grp_{n}{b}{h}", tag="grp", bufs=6, align_bytes=64)
-            return grp[n, b, h]
+        def grouped(n, o):
+            if (n, o) not in grp:
+                grp[n, o] = keep.tile([P, 4096], BF16, name=f"grp_{n}{o}", tag="grp", bufs=GRP_BUFS, align_bytes=64)
+            return grp[n, o]
 
         def bank(dtype=F32, cols=512):
             return psum.tile([P, cols], dtype, name="bank", tag="bank")
@@ -70,6 +70,10 @@ def tile_localattention_pa_v_kernel(tc, x, Wq, bq, k, p, grad_out, out_0, out_1)
                 nc.vector.tensor_copy(out=out, in_=in_)
             else:
                 nc.scalar.copy(out=out, in_=in_)
+
+        def empty(eng, *jobs):
+            for job in reversed(jobs):
+                job(eng)
 
         def load_window(b, i0=0, i1=4):
             step = P * S + WIN_STEP
@@ -118,42 +122,41 @@ def tile_localattention_pa_v_kernel(tc, x, Wq, bq, k, p, grad_out, out_0, out_1)
                 for u in range(2):
                     at = 256 * u + 128 * i
                     nc.tensor.transpose(t[:, at : at + 128], words[:, u : S // 2 : 2], ident[:])
-            return t
-
-        def take_dz(b, h, t, eng):
             words = dzg[b][:].bitcast(F32).rearrange("p (t m u) -> p t m u", t=4, u=2)
-            copy(eng, words[:, :, 64 * h : 64 * (h + 1), :], t[:].rearrange("p (u m t) -> p t m u", u=2, t=4))
+            return lambda eng: copy(eng, words[:, :, 64 * h : 64 * (h + 1), :], t[:].rearrange("p (u m t) -> p t m u", u=2, t=4))
 
         def quant_dz(b):
             nc.vector.quantize_mx(out=dzc[b][:].bitcast(E5M2), scales=dzs[b][:], in_=dzg[b][:])
 
+        def home(n, b, h):
+            return (b, h) if n == "k" else (h, b)
+
+        def woven(n, b, h):
+            o, i = home(n, b, h)
+            return grouped(n, o)[:, 2048 * i : 2048 * (i + 1)]
+
         def weave_pe(n, b, h, a):
-            src = raw[n, b, h]
             t = bank(BF16, 1024)
             for c in range(2):
                 cols = slice(256 * a + P * c, 256 * a + P * (c + 1))
-                nc.tensor.matmul(t[:, 512 * c : 512 * (c + 1)], lhsT=ident_bf[:], rhs=src[:, :, cols].rearrange("p j c -> p c j"), start=True, stop=True)
-            return t
+                nc.tensor.matmul(t[:, 512 * c : 512 * (c + 1)], lhsT=ident_bf[:], rhs=raw[n, b, h][:, :, cols].rearrange("p j c -> p c j"), start=True, stop=True)
+            if n == "k":
+                dst = woven(n, b, h).rearrange("p (t m j) -> p t m j", t=4, j=4)[:, :, 64 * a : 64 * (a + 1), :]
+                return lambda eng: copy(eng, dst, t[:].rearrange("p (m t j) -> p t m j", t=4, j=4))
+            dst = woven(n, b, h)[:, 1024 * a : 1024 * (a + 1)]
+            return lambda eng: copy(eng, dst, t[:])
 
-        def take_k(b, g, a, t, eng):
-            dst = grouped("k", b, g)[:].rearrange("p (t m j) -> p t m j", t=4, j=4)[:, :, 64 * a : 64 * (a + 1), :]
-            copy(eng, dst, t[:].rearrange("p (m t j) -> p t m j", t=4, j=4))
+        def weave_k(b, g, a0=0, a1=2):
+            dst = woven("k", b, g).rearrange("p (t m j) -> p t m j", t=4, j=4)[:, :, 64 * a0 : 64 * a1, :]
+            nc.vector.tensor_copy(out=dst.rearrange("p t (n i) j -> p n t i j", i=2), in_=raw["k", b, g][:, :, 256 * a0 : 256 * a1].rearrange("p j (n i t) -> p n t i j", i=2, t=4))
 
-        def weave_k(b, g, a, eng):
-            src = raw["k", b, g]
-            dst = grouped("k", b, g)[:].rearrange("p (t m j) -> p t m j", t=4, j=4)[:, :, 64 * a : 64 * (a + 1), :]
-            copy(eng, dst.rearrange("p t (n i) j -> p n t i j", i=2), src[:, :, 256 * a : 256 * (a + 1)].rearrange("p j (n i t) -> p n t i j", i=2, t=4))
+        def weave(n, b, h, a0=0, a1=2, eng=V):
+            dst = woven(n, b, h)[:, 1024 * a0 : 1024 * a1].rearrange("p (c i t) -> p c t i", i=4, t=4)
+            copy(eng, dst, raw[n, b, h][:, :, 256 * a0 : 256 * a1].rearrange("p t (c i) -> p c t i", i=4))
 
-        def weave(n, b, h, a, eng):
-            dst = grouped(n, b, h)[:, 1024 * a : 1024 * (a + 1)].rearrange("p (c i t) -> p c t i", i=4, t=4)
-            copy(eng, dst, raw[n, b, h][:, :, 256 * a : 256 * (a + 1)].rearrange("p t (c i) -> p c t i", i=4))
-
-        def take_woven(n, b, h, a, t, eng):
-            copy(eng, grouped(n, b, h)[:, 1024 * a : 1024 * (a + 1)], t[:])
-
-        def quant(n, b, h):
-            cols = slice(512 * h, 512 * (h + 1))
-            nc.vector.quantize_mx(out=code[n][b][:, cols].bitcast(E4M3), scales=scale[n][b][:, cols], in_=grouped(n, b, h)[:])
+        def quant(n, o, c0=0, c1=4):
+            cols = slice(256 * c0, 256 * c1)
+            nc.vector.quantize_mx(out=code[n][o][:, cols].bitcast(E4M3), scales=scale[n][o][:, cols], in_=grouped(n, o)[:, 1024 * c0 : 1024 * c1])
 
         def kop(b, s):
             cols = slice(P * s, P * (s + 1))
@@ -177,28 +180,69 @@ def tile_localattention_pa_v_kernel(tc, x, Wq, bq, k, p, grad_out, out_0, out_1)
             else:
                 nc.vector.tensor_scalar(out=dst, in0=src, scalar1=1.0 / 32.0, scalar2=None, op0=MULT)
 
-        def dqa(b, t, g, eng):
+        def dqa(b, t, g):
             o = four([(kop(b, 4 * g + j), zop(b, t)) for j in range(4)])
-            take_dq(dq["a"][4 * b + t][:, 512 * g : 512 * (g + 1)], o, eng)
+            at = 1024 * t + 512 * g
+            return lambda eng: take_dq(dq["a"][b][:, at : at + 512], o, eng)
 
-        def dqb(s, b, eng):
+        def dqb(s, b):
             o = four([(zop(b, j), kop(b, s)) for j in range(4)])
-            take_dq(dq["b"][s][:, 512 * b : 512 * (b + 1)], o, eng)
+            at = 1024 * (s % 4) + 512 * b
+            return lambda eng: take_dq(dq["b"][s // 4][:, at : at + 512], o, eng)
 
-        def quant_dq(n, i):
-            nc.vector.quantize_mx(out=dqc[n][i][:].bitcast(E5M2), scales=dqs[n][i][:], in_=dq[n][i][:])
+        def quant_dq(n, i0, i1):
+            g, t0, t1 = i0 // 4, i0 % 4, (i1 - 1) % 4 + 1
+            cols = slice(256 * t0, 256 * t1)
+            nc.vector.quantize_mx(out=dqc[n][g][:, cols].bitcast(E5M2), scales=dqs[n][g][:, cols], in_=dq[n][g][:, 1024 * t0 : 1024 * t1])
 
-        def product(n, i, h, eng):
+        def product(n, i, h, dst=None):
             other = {"a": "w", "b": "x"}[n]
-            if (n, i) not in res:
-                res[n, i] = outs.tile([P, 1024], F32, name="res", tag="res")
             o = bank()
-            cols = slice(512 * h, 512 * (h + 1))
             for g in range(2):
-                mine = slice(P * g, P * (g + 1))
-                nc.tensor.matmul_mx(out=o[:], lhsT=dqc[n][i][:, mine].bitcast(E5M2), lhsT_scale=dqs[n][i][:, mine],
-                                    rhs=code[other][g][:, cols].bitcast(E4M3), rhs_scale=scale[other][g][:, cols], start=(g == 0), stop=(g == 1))
-            copy(eng, res[n, i][:, cols], o[:])
+                mine = slice(256 * (i % 4) + P * g, 256 * (i % 4) + P * (g + 1))
+                cols = slice(512 * g, 512 * (g + 1))
+                nc.tensor.matmul_mx(out=o[:], lhsT=dqc[n][i // 4][:, mine].bitcast(E5M2), lhsT_scale=dqs[n][i // 4][:, mine],
+                                    rhs=code[other][h][:, cols].bitcast(E4M3), rhs_scale=scale[other][h][:, cols], start=(g == 0), stop=(g == 1))
+
+            def take(eng):
+                if dst is not None:
+                    return copy(eng, dst, o[:])
+                if (n, i) not in res:
+                    res[n, i] = outs.tile([P, 1024], F32, name="res", tag="res")
+                copy(eng, res[n, i][:, 512 * h : 512 * (h + 1)], o[:])
+
+            return take
+
+        def quarter(n, i, h, a):
+            other = {"a": "w", "b": "x"}[n]
+            o = bank()
+            for j in range(2):
+                for g in range(2):
+                    mine = slice(256 * (i % 4 + j) + P * g, 256 * (i % 4 + j) + P * (g + 1))
+                    cols = slice(512 * g + 256 * a, 512 * g + 256 * (a + 1))
+                    nc.tensor.matmul_mx(out=o[:, 256 * j : 256 * (j + 1)], lhsT=dqc[n][i // 4][:, mine].bitcast(E5M2), lhsT_scale=dqs[n][i // 4][:, mine],
+                                        rhs=code[other][h][:, cols].bitcast(E4M3), rhs_scale=scale[other][h][:, cols], start=(g == 0), stop=(g == 1))
+
+            def take(eng):
+                out = outs.tile([P, 2, 256], F32, name="res", tag="res")
+                copy(eng, out[:].rearrange("p j c -> p (j c)"), o[:])
+                g, t = divmod(i, 4)
+                dst = out_0[g] if n == "a" else out_1[512 * g : 512 * (g + 1), :]
+                nc.sync.dma_start(out=dst.rearrange("(m t) d -> m t d", t=4)[:, t : t + 2, 512 * h + 256 * a : 512 * h + 256 * (a + 1)], in_=out[:])
+
+            return take
+
+        def halves(n, i, h, eng=A):
+            out = outs.tile([P, 2, 512], F32, name="res", tag="res")
+            jobs = [product(n, i + j, h, out[:, j, :]) for j in range(2)]
+            empty(eng, *jobs)
+            g, t = divmod(i, 4)
+            dst = out_0[g] if n == "a" else out_1[512 * g : 512 * (g + 1), :]
+            nc.sync.dma_start(out=dst.rearrange("(m t) d -> m t d", t=4)[:, t : t + 2, 512 * h : 512 * (h + 1)], in_=out[:])
+
+        def whole(n, i, eng=A):
+            empty(eng, product(n, i, 0), product(n, i, 1))
+            store(n, i)
 
         def store(n, i, h=None):
             cols = slice(0, 1024) if h is None else slice(512 * h, 512 * (h + 1))
@@ -210,101 +254,85 @@ def tile_localattention_pa_v_kernel(tc, x, Wq, bq, k, p, grad_out, out_0, out_1)
         make_identity(nc, ident_bf[:])
         for b in range(B):
             for i in range(4):
-                nc.vector.memset(dz[b][i][:], 0.0)
-        load_window(0)
+                nc.vector.memset(dz[b][i][:].bitcast(F32), 0.0)
+        load_window(0, 0, 2)
+        load_window(0, 2, 4)
         load_half("k", 0, 0)
         load_half("k", 0, 1)
         load_half("w", 0, 0)
         load_half("w", 1, 0)
         load_window(1)
+        load("k", 1)
         load_half("w", 0, 1)
         load_half("w", 1, 1)
-        load("k", 1)
         load("x", 0)
         load("x", 1)
-        row_sums(0, range(4))
-        soft(0, range(4))
         for h in range(2):
-            take_dz(0, h, turn_dz(0, h), A)
+            row_sums(0, (2 * h, 2 * h + 1))
+            soft(0, (2 * h, 2 * h + 1))
+            empty(A, turn_dz(0, h))
+        weave_k(0, 0)
         for a in range(2):
-            weave_k(0, 0, a, V)
-        for a in range(2):
-            take_k(0, 1, a, weave_pe("k", 0, 1, a), A)
-        quant("k", 0, 0)
+            empty(A, weave_pe("k", 0, 1, a))
+        quant("k", 0, 0, 2)
         quant_dz(0)
-        for t in range(4):
-            dqa(0, t, 0, A)
-        weave("w", 0, 0, 0, V)
-        weave("w", 0, 0, 1, V)
-        quant("k", 0, 1)
-        for t in range(4):
-            dqa(0, t, 1, A)
-        weave("w", 1, 0, 0, V)
-        weave("w", 1, 0, 1, V)
-        quant("w", 0, 0)
-        quant_dq("a", 0)
-        quant("w", 1, 0)
-        quant_dq("a", 1)
+        empty(A, dqa(0, 0, 0), dqa(0, 1, 0))
+        empty(A, dqa(0, 2, 0), dqa(0, 3, 0))
+        weave("w", 0, 0)
+        weave("w", 1, 0)
+        quant("k", 0, 2, 4)
+        empty(A, dqa(0, 0, 1), dqa(0, 1, 1))
+        empty(A, dqa(0, 2, 1), dqa(0, 3, 1))
+        quant("w", 0)
         row_sums(1, range(4))
-        quant_dq("a", 2)
         soft(1, range(4))
-        quant_dq("a", 3)
-        dqb(0, 0, A)
-        for t in range(4):
-            product("a", t, 0, A)
-            store("a", t, 0)
-            dqb(t + 1, 0, A)
-        for h in range(2):
-            take_dz(1, h, turn_dz(1, h), A)
-        for t in range(4):
-            weave("w", t // 2, 1, t % 2, V)
-        quant("w", 0, 1)
-        weave_k(1, 0, 0, V)
-        quant("w", 1, 1)
-        for s in range(5, 8):
-            dqb(s, 0, A)
-        for t in range(4):
-            product("a", t, 1, A)
-            store("a", t, 1)
-        weave_k(1, 0, 1, V)
+        quant_dq("a", 0, 2)
+        weave_k(1, 0)
+        quant_dq("a", 2, 4)
+        weave_k(1, 1)
+        empty(A, dqb(0, 0), dqb(1, 0))
+        empty(A, turn_dz(1, 0), turn_dz(1, 1))
+        halves("a", 0, 0)
         quant_dz(1)
-        quant("k", 1, 0)
-        for t in range(4):
-            dqa(1, t, 0, A)
-        weave_k(1, 1, 0, V)
-        weave_k(1, 1, 1, V)
-        weave("x", 0, 0, 0, V)
-        quant("k", 1, 1)
-        for t in range(4):
-            dqa(1, t, 1, A)
-        weave("x", 0, 0, 1, V)
-        weave("x", 1, 0, 0, V)
-        quant_dq("a", 4)
-        weave("x", 1, 0, 1, V)
-        quant_dq("a", 5)
-        quant("x", 0, 0)
-        quant_dq("a", 6)
-        quant("x", 1, 0)
-        quant_dq("a", 7)
-        for t in range(4):
-            dqb(t, 1, V)
-            for h in range(2):
-                product("a", 4 + t, h, A)
-            store("a", 4 + t)
-            if t > 0:
-                quant_dq("b", t - 1)
-        dqb(4, 1, V)
-        quant_dq("b", 3)
-        for s in range(8):
-            if s < 3:
-                dqb(5 + s, 1, A)
-            if s < 4:
-                weave("x", s // 2, 1, s % 2, V)
-                quant_dq("b", 4 + s)
-            if s in (4, 5):
-                quant("x", s - 4, 1)
-            product("b", s, 0, A)
-            store("b", s, 0)
-        for s in range(8):
-            product("b", s, 1, (A, V)[s % 2])
-            store("b", s, 1)
+        quant("k", 1)
+        empty(A, dqb(2, 0), dqb(3, 0))
+        halves("a", 2, 0)
+        weave("w", 0, 1)
+        empty(A, dqb(4, 0), dqb(5, 0))
+        empty(V, dqa(1, 0, 0), dqa(1, 0, 1))
+        empty(A, dqb(6, 0), dqb(7, 0))
+        empty(A, dqa(1, 1, 0), dqa(1, 1, 1))
+        weave("w", 1, 1)
+        empty(A, dqa(1, 2, 0), dqa(1, 2, 1))
+        quant_dq("a", 4, 6)
+        quant("w", 1)
+        empty(V, dqa(1, 3, 0), dqa(1, 3, 1))
+        empty(A, dqb(0, 1), dqb(1, 1))
+        halves("a", 4, 0)
+        weave("x", 0, 0)
+        quant_dq("a", 6, 8)
+        halves("a", 0, 1)
+        empty(A, dqb(2, 1), dqb(3, 1))
+        weave("x", 1, 0)
+        halves("a", 2, 1)
+        quant_dq("b", 0, 4)
+        quant("x", 0)
+        empty(V, dqb(4, 1), dqb(5, 1))
+        halves("a", 4, 1)
+        empty(A, dqb(6, 1), dqb(7, 1))
+        whole("a", 6)
+        whole("a", 7)
+        weave("x", 0, 1, 0, 1)
+        weave("x", 1, 1, 0, 1)
+        quant_dq("b", 4, 8)
+        quant("x", 1, 0, 1)
+        quant("x", 1, 2, 3)
+        weave("x", 0, 1, 1, 2)
+        weave("x", 1, 1, 1, 2)
+        quant("x", 1, 1, 2)
+        quant("x", 1, 3, 4)
+        for s in range(0, 8, 2):
+            halves("b", s, 0)
+        for a in range(2):
+            for s in range(0, 8, 2):
+                empty((A, V)[(s // 2) % 2], quarter("b", s, 1, a))

@@ -259,12 +259,10 @@ def tile_localattention_pa_v_kernel(tc, x, Wq, bq, k, p, grad_out, out_0, out_1)
         load_window(0, 2, 4)
         load_half("k", 0, 0)
         load_half("k", 0, 1)
-        load_half("w", 0, 0)
-        load_half("w", 1, 0)
         load_window(1)
         load("k", 1)
-        load_half("w", 0, 1)
-        load_half("w", 1, 1)
+        load("w", 0)
+        load("w", 1)
         load("x", 0)
         load("x", 1)
         for h in range(2):
@@ -276,63 +274,64 @@ def tile_localattention_pa_v_kernel(tc, x, Wq, bq, k, p, grad_out, out_0, out_1)
             empty(A, weave_pe("k", 0, 1, a))
         quant("k", 0, 0, 2)
         quant_dz(0)
-        empty(A, dqa(0, 0, 0), dqa(0, 1, 0))
-        empty(A, dqa(0, 2, 0), dqa(0, 3, 0))
-        weave("w", 0, 0)
-        weave("w", 1, 0)
-        quant("k", 0, 2, 4)
-        empty(A, dqa(0, 0, 1), dqa(0, 1, 1))
-        empty(A, dqa(0, 2, 1), dqa(0, 3, 1))
-        quant("w", 0)
         row_sums(1, range(4))
         soft(1, range(4))
-        quant_dq("a", 0, 2)
-        weave_k(1, 0)
-        quant_dq("a", 2, 4)
-        weave_k(1, 1)
-        empty(A, dqb(0, 0), dqb(1, 0))
+        quant("k", 0, 2, 4)
+        empty(A, dqa(0, 0, 0), dqa(0, 1, 0))
+        empty(A, dqa(0, 2, 0), dqa(0, 3, 0))
         empty(A, turn_dz(1, 0), turn_dz(1, 1))
-        halves("a", 0, 0)
+        weave_k(1, 0)
+        weave_k(1, 1)
         quant_dz(1)
         quant("k", 1)
+        empty(A, dqa(0, 0, 1), dqa(0, 1, 1))
+        empty(A, dqa(0, 2, 1), dqa(0, 3, 1))
+        empty(A, dqb(0, 0), dqb(1, 0))
         empty(A, dqb(2, 0), dqb(3, 0))
+        weave("w", 0, 0)
+        weave("w", 1, 0)
+        quant_dq("a", 0, 4)
+        quant("w", 0)
+        for t in range(4):
+            empty(A, dqa(1, t, 0), dqa(1, t, 1))
+        halves("a", 0, 0)
         halves("a", 2, 0)
         weave("w", 0, 1)
-        empty(A, dqb(4, 0), dqb(5, 0))
-        empty(V, dqa(1, 0, 0), dqa(1, 0, 1))
-        empty(A, dqb(6, 0), dqb(7, 0))
-        empty(A, dqa(1, 1, 0), dqa(1, 1, 1))
-        weave("w", 1, 1)
-        empty(A, dqa(1, 2, 0), dqa(1, 2, 1))
         quant_dq("a", 4, 6)
-        quant("w", 1)
-        empty(V, dqa(1, 3, 0), dqa(1, 3, 1))
-        empty(A, dqb(0, 1), dqb(1, 1))
-        halves("a", 4, 0)
-        weave("x", 0, 0)
+        weave("w", 1, 1)
         quant_dq("a", 6, 8)
-        halves("a", 0, 1)
-        empty(A, dqb(2, 1), dqb(3, 1))
+        quant("w", 1)
+        halves("a", 4, 0)
+        halves("a", 6, 0)
+        weave("x", 0, 0)
         weave("x", 1, 0)
-        halves("a", 2, 1)
-        quant_dq("b", 0, 4)
+        weave("x", 0, 1)
         quant("x", 0)
-        empty(V, dqb(4, 1), dqb(5, 1))
+        halves("a", 0, 1)
+        halves("a", 2, 1)
+        empty(A, dqb(0, 1), dqb(1, 1))
         halves("a", 4, 1)
-        empty(A, dqb(6, 1), dqb(7, 1))
-        whole("a", 6)
-        whole("a", 7)
-        weave("x", 0, 1, 0, 1)
-        weave("x", 1, 1, 0, 1)
-        quant_dq("b", 4, 8)
-        quant("x", 1, 0, 1)
-        quant("x", 1, 2, 3)
-        weave("x", 0, 1, 1, 2)
-        weave("x", 1, 1, 1, 2)
-        quant("x", 1, 1, 2)
-        quant("x", 1, 3, 4)
-        for s in range(0, 8, 2):
-            halves("b", s, 0)
-        for a in range(2):
-            for s in range(0, 8, 2):
-                empty((A, V)[(s // 2) % 2], quarter("b", s, 1, a))
+        halves("a", 6, 1)
+        quant_dq("b", 0, 2)
+        weave("x", 1, 1)
+        empty(A, dqb(2, 1), dqb(3, 1))
+        halves("b", 0, 0)
+        quant("x", 1)
+        quant_dq("b", 2, 4)
+        empty(A, dqb(4, 0), dqb(4, 1))
+        empty(V, dqb(5, 0), dqb(5, 1))
+        quant_dq("b", 4, 5)
+        empty(V, dqb(6, 0), dqb(6, 1))
+        halves("b", 0, 1)
+        quant_dq("b", 5, 6)
+        whole("b", 2)
+        empty(V, dqb(7, 0), dqb(7, 1))
+        quant_dq("b", 6, 7)
+        whole("b", 3)
+        quant_dq("b", 7, 8)
+        whole("b", 4)
+        whole("b", 5, V)
+        whole("b", 6)
+        for h in range(2):
+            empty((V, A)[h], product("b", 7, h))
+            store("b", 7, h)

@@ -32,7 +32,7 @@ def tile_localattention_pa_v_kernel(tc, x, Wq, bq, k, p, grad_out, out_0, out_1)
     with ExitStack() as ctx:
         keep = ctx.enter_context(tc.tile_pool(name="keep", bufs=1))
         outs = ctx.enter_context(tc.tile_pool(name="outs", bufs=10))
-        psum = ctx.enter_context(tc.psum_pool(name="psum", bufs=8))
+        psum = ctx.enter_context(tc.psum_pool(name="psum", bufs=1))
         ctx.enter_context(tc.manual_schedule())
 
         def tiles(name, shape, dtype, n=2):
@@ -60,8 +60,12 @@ def tile_localattention_pa_v_kernel(tc, x, Wq, bq, k, p, grad_out, out_0, out_1)
                 grp[n, o] = keep.tile([P, 4096], BF16, name=f"grp_{n}{o}", tag="grp", bufs=GRP_BUFS, align_bytes=64)
             return grp[n, o]
 
+        spare = list(range(8))
+
         def bank(dtype=F32, cols=512):
-            return psum.tile([P, cols], dtype, name="bank", tag="bank")
+            n = spare[0]
+            spare.remove(n)
+            return n, psum.tile([P, cols], dtype, name=f"bank{n}", tag=f"bank{n}")
 
         V, A = "V", "A"
 
@@ -72,8 +76,9 @@ def tile_localattention_pa_v_kernel(tc, x, Wq, bq, k, p, grad_out, out_0, out_1)
                 nc.scalar.copy(out=out, in_=in_)
 
         def empty(eng, *jobs):
-            for job in reversed(jobs):
+            for n, job in reversed(jobs):
                 job(eng)
+                spare.append(n)
 
         def load_window(b, i0=0, i1=4):
             step = P * S + WIN_STEP
@@ -116,14 +121,14 @@ def tile_localattention_pa_v_kernel(tc, x, Wq, bq, k, p, grad_out, out_0, out_1)
                 nc.vector.scalar_tensor_tensor(out=dz[b][i][:, cols], in0=gw[b][:, i, w], scalar=rsum[b][:, i : i + 1], in1=pw[b][:, i, w], op0=SUB, op1=MULT)
 
         def turn_dz(b, h):
-            t = bank()
+            n, t = bank()
             for i in range(2):
                 words = dz[b][2 * h + i][:].bitcast(F32)
                 for u in range(2):
                     at = 256 * u + 128 * i
                     nc.tensor.transpose(t[:, at : at + 128], words[:, u : S // 2 : 2], ident[:])
             words = dzg[b][:].bitcast(F32).rearrange("p (t m u) -> p t m u", t=4, u=2)
-            return lambda eng: copy(eng, words[:, :, 64 * h : 64 * (h + 1), :], t[:].rearrange("p (u m t) -> p t m u", u=2, t=4))
+            return n, lambda eng: copy(eng, words[:, :, 64 * h : 64 * (h + 1), :], t[:].rearrange("p (u m t) -> p t m u", u=2, t=4))
 
         def quant_dz(b):
             nc.vector.quantize_mx(out=dzc[b][:].bitcast(E5M2), scales=dzs[b][:], in_=dzg[b][:])
@@ -136,15 +141,15 @@ def tile_localattention_pa_v_kernel(tc, x, Wq, bq, k, p, grad_out, out_0, out_1)
             return grouped(n, o)[:, 2048 * i : 2048 * (i + 1)]
 
         def weave_pe(n, b, h, a):
-            t = bank(BF16, 1024)
+            slot, t = bank(BF16, 1024)
             for c in range(2):
                 cols = slice(256 * a + P * c, 256 * a + P * (c + 1))
                 nc.tensor.matmul(t[:, 512 * c : 512 * (c + 1)], lhsT=ident_bf[:], rhs=raw[n, b, h][:, :, cols].rearrange("p j c -> p c j"), start=True, stop=True)
             if n == "k":
                 dst = woven(n, b, h).rearrange("p (t m j) -> p t m j", t=4, j=4)[:, :, 64 * a : 64 * (a + 1), :]
-                return lambda eng: copy(eng, dst, t[:].rearrange("p (m t j) -> p t m j", t=4, j=4))
+                return slot, lambda eng: copy(eng, dst, t[:].rearrange("p (m t j) -> p t m j", t=4, j=4))
             dst = woven(n, b, h)[:, 1024 * a : 1024 * (a + 1)]
-            return lambda eng: copy(eng, dst, t[:])
+            return slot, lambda eng: copy(eng, dst, t[:])
 
         def weave_k(b, g, a0=0, a1=2):
             dst = woven("k", b, g).rearrange("p (t m j) -> p t m j", t=4, j=4)[:, :, 64 * a0 : 64 * a1, :]
@@ -167,10 +172,10 @@ def tile_localattention_pa_v_kernel(tc, x, Wq, bq, k, p, grad_out, out_0, out_1)
             return dzc[b][:, cols].bitcast(E5M2), dzs[b][:, cols]
 
         def four(pairs):
-            o = bank()
+            n, o = bank()
             for t, (still, moving) in enumerate(pairs):
                 nc.tensor.matmul_mx(out=o[:, P * t : P * (t + 1)], lhsT=still[0], lhsT_scale=still[1], rhs=moving[0], rhs_scale=moving[1], start=True, stop=True)
-            return o
+            return n, o
 
         def take_dq(dst, o, eng):
             dst = dst.rearrange("p (c t) -> p c t", t=4)
@@ -181,14 +186,14 @@ def tile_localattention_pa_v_kernel(tc, x, Wq, bq, k, p, grad_out, out_0, out_1)
                 nc.vector.tensor_scalar(out=dst, in0=src, scalar1=1.0 / 32.0, scalar2=None, op0=MULT)
 
         def dqa(b, t, g):
-            o = four([(kop(b, 4 * g + j), zop(b, t)) for j in range(4)])
+            n, o = four([(kop(b, 4 * g + j), zop(b, t)) for j in range(4)])
             at = 1024 * t + 512 * g
-            return lambda eng: take_dq(dq["a"][b][:, at : at + 512], o, eng)
+            return n, lambda eng: take_dq(dq["a"][b][:, at : at + 512], o, eng)
 
         def dqb(s, b):
-            o = four([(zop(b, j), kop(b, s)) for j in range(4)])
+            n, o = four([(zop(b, j), kop(b, s)) for j in range(4)])
             at = 1024 * (s % 4) + 512 * b
-            return lambda eng: take_dq(dq["b"][s // 4][:, at : at + 512], o, eng)
+            return n, lambda eng: take_dq(dq["b"][s // 4][:, at : at + 512], o, eng)
 
         def quant_dq(n, i0, i1):
             g, t0, t1 = i0 // 4, i0 % 4, (i1 - 1) % 4 + 1
@@ -197,7 +202,7 @@ def tile_localattention_pa_v_kernel(tc, x, Wq, bq, k, p, grad_out, out_0, out_1)
 
         def product(n, i, h, dst=None):
             other = {"a": "w", "b": "x"}[n]
-            o = bank()
+            slot, o = bank()
             for g in range(2):
                 mine = slice(256 * (i % 4) + P * g, 256 * (i % 4) + P * (g + 1))
                 cols = slice(512 * g, 512 * (g + 1))
@@ -211,11 +216,11 @@ def tile_localattention_pa_v_kernel(tc, x, Wq, bq, k, p, grad_out, out_0, out_1)
                     res[n, i] = outs.tile([P, 1024], F32, name="res", tag="res")
                 copy(eng, res[n, i][:, 512 * h : 512 * (h + 1)], o[:])
 
-            return take
+            return slot, take
 
         def quarter(n, i, h, a):
             other = {"a": "w", "b": "x"}[n]
-            o = bank()
+            slot, o = bank()
             for j in range(2):
                 for g in range(2):
                     mine = slice(256 * (i % 4 + j) + P * g, 256 * (i % 4 + j) + P * (g + 1))
@@ -230,18 +235,22 @@ def tile_localattention_pa_v_kernel(tc, x, Wq, bq, k, p, grad_out, out_0, out_1)
                 dst = out_0[g] if n == "a" else out_1[512 * g : 512 * (g + 1), :]
                 nc.sync.dma_start(out=dst.rearrange("(m t) d -> m t d", t=4)[:, t : t + 2, 512 * h + 256 * a : 512 * h + 256 * (a + 1)], in_=out[:])
 
-            return take
+            return slot, take
 
-        def halves(n, i, h, eng=A):
+        def halves(n, i, h, eng=A, paired=True):
             out = outs.tile([P, 2, 512], F32, name="res", tag="res")
             jobs = [product(n, i + j, h, out[:, j, :]) for j in range(2)]
-            empty(eng, *jobs)
+            empty(eng, *(jobs if paired else reversed(jobs)))
             g, t = divmod(i, 4)
             dst = out_0[g] if n == "a" else out_1[512 * g : 512 * (g + 1), :]
             nc.sync.dma_start(out=dst.rearrange("(m t) d -> m t d", t=4)[:, t : t + 2, 512 * h : 512 * (h + 1)], in_=out[:])
 
-        def whole(n, i, eng=A):
-            empty(eng, product(n, i, 0), product(n, i, 1))
+        def whole(n, i, eng=A, other=None):
+            if other is None:
+                empty(eng, product(n, i, 0), product(n, i, 1))
+            else:
+                empty(eng, product(n, i, 0))
+                empty(other, product(n, i, 1))
             store(n, i)
 
         def store(n, i, h=None):
@@ -294,6 +303,7 @@ def tile_localattention_pa_v_kernel(tc, x, Wq, bq, k, p, grad_out, out_0, out_1)
         quant("w", 0)
         for t in range(4):
             empty(A, dqa(1, t, 0), dqa(1, t, 1))
+        early = [dqb(s, 1) for s in range(2)]
         halves("a", 0, 0)
         halves("a", 2, 0)
         weave("w", 0, 1)
@@ -302,6 +312,7 @@ def tile_localattention_pa_v_kernel(tc, x, Wq, bq, k, p, grad_out, out_0, out_1)
         quant_dq("a", 6, 8)
         quant("w", 1)
         halves("a", 4, 0)
+        empty(A, *early)
         halves("a", 6, 0)
         weave("x", 0, 0)
         weave("x", 1, 0)
@@ -309,29 +320,32 @@ def tile_localattention_pa_v_kernel(tc, x, Wq, bq, k, p, grad_out, out_0, out_1)
         quant("x", 0)
         halves("a", 0, 1)
         halves("a", 2, 1)
-        empty(A, dqb(0, 1), dqb(1, 1))
+        empty(A, dqb(2, 1), dqb(3, 1))
         halves("a", 4, 1)
         halves("a", 6, 1)
+        late = {4: [dqb(4, b) for b in range(2)]}
         quant_dq("b", 0, 2)
         weave("x", 1, 1)
-        empty(A, dqb(2, 1), dqb(3, 1))
-        halves("b", 0, 0)
-        quant("x", 1)
         quant_dq("b", 2, 4)
-        empty(A, dqb(4, 0), dqb(4, 1))
-        empty(V, dqb(5, 0), dqb(5, 1))
+        quant("x", 1)
+        halves("b", 0, 0)
+        late[5] = [dqb(5, b) for b in range(2)]
+        halves("b", 2, 0, A, False)
+        empty(V, *late[4])
+        halves("b", 0, 1, A, False)
+        empty(V, *late[5])
         quant_dq("b", 4, 5)
-        empty(V, dqb(6, 0), dqb(6, 1))
-        halves("b", 0, 1)
+        late[6] = [dqb(6, b) for b in range(2)]
+        halves("b", 2, 1, A, False)
+        empty(V, *late[6])
         quant_dq("b", 5, 6)
-        whole("b", 2)
-        empty(V, dqb(7, 0), dqb(7, 1))
+        late[7] = [dqb(7, b) for b in range(2)]
+        whole("b", 4, A, A)
+        empty(V, *late[7])
         quant_dq("b", 6, 7)
-        whole("b", 3)
+        whole("b", 5, A, A)
         quant_dq("b", 7, 8)
-        whole("b", 4)
-        whole("b", 5, V)
-        whole("b", 6)
+        whole("b", 6, A, V)
         for h in range(2):
-            empty((V, A)[h], product("b", 7, h))
+            empty((A, V)[h], product("b", 7, h))
             store("b", 7, h)

@@ -51,7 +51,9 @@ def tile_localattention_pa_v_kernel(tc, x, Wq, bq, k, p, grad_out, out_0, out_1)
         raw, grp, res = {}, {}, {}
         code = {n: tiles(n + "code", [P, 1024], U32) for n in ("k", "w", "x")}
         scale = {n: tiles(n + "scale", [P, 1024], U8) for n in ("k", "w", "x")}
-        dq = {n: tiles("dq" + n, [P, 4096], BF16) for n in ("a", "b")}
+        dqn = keep.tile([P, 8192], BF16, name="dqn", tag="dqn", align_bytes=64)
+        dq = {"a": tiles("dqa", [P, 4096], BF16)}
+        dqw = {}
         dqc = {n: tiles("dqc" + n, [P, 1024], U32) for n in ("a", "b")}
         dqs = {n: tiles("dqs" + n, [P, 1024], U8) for n in ("a", "b")}
 
@@ -78,7 +80,7 @@ def tile_localattention_pa_v_kernel(tc, x, Wq, bq, k, p, grad_out, out_0, out_1)
         def empty(eng, *jobs):
             for n, job in reversed(jobs):
                 job(eng)
-                spare.append(n)
+            spare.extend(n for n, job in jobs)
 
         def load_window(b, i0=0, i1=4):
             step = P * S + WIN_STEP
@@ -145,15 +147,8 @@ def tile_localattention_pa_v_kernel(tc, x, Wq, bq, k, p, grad_out, out_0, out_1)
             for c in range(2):
                 cols = slice(256 * a + P * c, 256 * a + P * (c + 1))
                 nc.tensor.matmul(t[:, 512 * c : 512 * (c + 1)], lhsT=ident_bf[:], rhs=raw[n, b, h][:, :, cols].rearrange("p j c -> p c j"), start=True, stop=True)
-            if n == "k":
-                dst = woven(n, b, h).rearrange("p (t m j) -> p t m j", t=4, j=4)[:, :, 64 * a : 64 * (a + 1), :]
-                return slot, lambda eng: copy(eng, dst, t[:].rearrange("p (m t j) -> p t m j", t=4, j=4))
             dst = woven(n, b, h)[:, 1024 * a : 1024 * (a + 1)]
             return slot, lambda eng: copy(eng, dst, t[:])
-
-        def weave_k(b, g, a0=0, a1=2):
-            dst = woven("k", b, g).rearrange("p (t m j) -> p t m j", t=4, j=4)[:, :, 64 * a0 : 64 * a1, :]
-            nc.vector.tensor_copy(out=dst.rearrange("p t (n i) j -> p n t i j", i=2), in_=raw["k", b, g][:, :, 256 * a0 : 256 * a1].rearrange("p j (n i t) -> p n t i j", i=2, t=4))
 
         def weave(n, b, h, a0=0, a1=2, eng=V):
             dst = woven(n, b, h)[:, 1024 * a0 : 1024 * a1].rearrange("p (c i t) -> p c t i", i=4, t=4)
@@ -163,48 +158,61 @@ def tile_localattention_pa_v_kernel(tc, x, Wq, bq, k, p, grad_out, out_0, out_1)
             cols = slice(256 * c0, 256 * c1)
             nc.vector.quantize_mx(out=code[n][o][:, cols].bitcast(E4M3), scales=scale[n][o][:, cols], in_=grouped(n, o)[:, 1024 * c0 : 1024 * c1])
 
-        def kop(b, s):
-            cols = slice(P * s, P * (s + 1))
-            return code["k"][b][:, cols].bitcast(E4M3), scale["k"][b][:, cols]
-
-        def zop(b, t):
-            cols = slice(P * t, P * (t + 1))
-            return dzc[b][:, cols].bitcast(E5M2), dzs[b][:, cols]
-
-        def four(pairs):
+        def dh(b, t, h):
             n, o = bank()
-            for t, (still, moving) in enumerate(pairs):
-                nc.tensor.matmul_mx(out=o[:, P * t : P * (t + 1)], lhsT=still[0], lhsT_scale=still[1], rhs=moving[0], rhs_scale=moving[1], start=True, stop=True)
-            return n, o
+            rows, cols = slice(P * t, P * (t + 1)), slice(512 * h, 512 * (h + 1))
+            nc.tensor.matmul_mx(out=o[:], lhsT=dzc[b][:, rows].bitcast(E5M2), lhsT_scale=dzs[b][:, rows],
+                                rhs=code["k"][b][:, cols].bitcast(E4M3), rhs_scale=scale["k"][b][:, cols], start=True, stop=True)
+            at = 4096 * b + 1024 * t + 512 * h
 
-        def take_dq(dst, o, eng):
-            dst = dst.rearrange("p (c t) -> p c t", t=4)
-            src = o[:].rearrange("p (t c) -> p c t", t=4)
-            if eng == A:
-                nc.scalar.activation(out=dst, in_=src, func=COPY, scale=1.0 / 32.0)
-            else:
-                nc.vector.tensor_scalar(out=dst, in0=src, scalar1=1.0 / 32.0, scalar2=None, op0=MULT)
+            dst = dqn[:, at : at + 512].rearrange("p (u w e) -> p u w e", u=2, e=2)
+            src = o[:].rearrange("p (w u e) -> p u w e", u=2, e=2)
 
-        def dqa(b, t, g):
-            n, o = four([(kop(b, 4 * g + j), zop(b, t)) for j in range(4)])
-            at = 1024 * t + 512 * g
-            return n, lambda eng: take_dq(dq["a"][b][:, at : at + 512], o, eng)
+            def take(eng):
+                if eng == A:
+                    nc.scalar.activation(out=dst, in_=src, func=COPY, scale=1.0 / 32.0)
+                else:
+                    nc.vector.tensor_scalar(out=dst, in0=src, scalar1=1.0 / 32.0, scalar2=None, op0=MULT)
 
-        def dqb(s, b):
-            n, o = four([(zop(b, j), kop(b, s)) for j in range(4)])
-            at = 1024 * (s % 4) + 512 * b
-            return n, lambda eng: take_dq(dq["b"][s // 4][:, at : at + 512], o, eng)
+            return n, take
 
-        def quant_dq(n, i0, i1):
+        def turn_dq(b, t):
+            n, o = bank()
+            words = dqn[:, 4096 * b + 1024 * t : 4096 * b + 1024 * (t + 1)].bitcast(F32)
+            for g in range(2):
+                for u in range(2):
+                    at = 256 * g + 128 * u
+                    nc.tensor.transpose(o[:, at : at + 128], words[:, at : at + 128], ident[:])
+            dst = dq["a"][b][:, 1024 * t : 1024 * (t + 1)].bitcast(F32).rearrange("p (g m u) -> p g m u", g=2, u=2)
+            return n, lambda eng: copy(eng, dst, o[:].rearrange("p (g u m) -> p g m u", g=2, u=2))
+
+        def quant_a(i0, i1):
             g, t0, t1 = i0 // 4, i0 % 4, (i1 - 1) % 4 + 1
             cols = slice(256 * t0, 256 * t1)
-            nc.vector.quantize_mx(out=dqc[n][g][:, cols].bitcast(E5M2), scales=dqs[n][g][:, cols], in_=dq[n][g][:, 1024 * t0 : 1024 * t1])
+            nc.vector.quantize_mx(out=dqc["a"][g][:, cols].bitcast(E5M2), scales=dqs["a"][g][:, cols], in_=dq["a"][g][:, 1024 * t0 : 1024 * t1])
+
+        def weave_dq(s):
+            dqw[s] = keep.tile([P, 1024], BF16, name=f"dqw{s}", tag="dqw", bufs=4, align_bytes=64)
+            src = dqn[:].rearrange("p (b t r w e) -> p r e b t w", b=2, t=4, r=4, e=2)[:, s // 2, s % 2]
+            nc.vector.tensor_copy(out=dqw[s][:].rearrange("p (b n i t) -> p b n t i", b=2, i=4, t=4), in_=src.rearrange("p b t (n i) -> p b n t i", i=4))
+
+        def quant_b(s):
+            cols = slice(256 * (s % 4), 256 * (s % 4 + 1))
+            nc.vector.quantize_mx(out=dqc["b"][s // 4][:, cols].bitcast(E5M2), scales=dqs["b"][s // 4][:, cols], in_=dqw[s][:])
+
+        def still(n, i, g):
+            at = 256 * (i % 4) + P * g
+            return slice(at, at + P)
+
+        def rows_out(n, i, count):
+            rows = out_0[i // 4] if n == "a" else out_1[512 * (i // 4) : 512 * (i // 4 + 1), :]
+            return rows.rearrange("(m t) d -> m t d", t=4)[:, i % 4 : i % 4 + count, :]
 
         def product(n, i, h, dst=None):
             other = {"a": "w", "b": "x"}[n]
             slot, o = bank()
             for g in range(2):
-                mine = slice(256 * (i % 4) + P * g, 256 * (i % 4) + P * (g + 1))
+                mine = still(n, i, g)
                 cols = slice(512 * g, 512 * (g + 1))
                 nc.tensor.matmul_mx(out=o[:], lhsT=dqc[n][i // 4][:, mine].bitcast(E5M2), lhsT_scale=dqs[n][i // 4][:, mine],
                                     rhs=code[other][h][:, cols].bitcast(E4M3), rhs_scale=scale[other][h][:, cols], start=(g == 0), stop=(g == 1))
@@ -218,32 +226,17 @@ def tile_localattention_pa_v_kernel(tc, x, Wq, bq, k, p, grad_out, out_0, out_1)
 
             return slot, take
 
-        def quarter(n, i, h, a):
-            other = {"a": "w", "b": "x"}[n]
-            slot, o = bank()
-            for j in range(2):
-                for g in range(2):
-                    mine = slice(256 * (i % 4 + j) + P * g, 256 * (i % 4 + j) + P * (g + 1))
-                    cols = slice(512 * g + 256 * a, 512 * g + 256 * (a + 1))
-                    nc.tensor.matmul_mx(out=o[:, 256 * j : 256 * (j + 1)], lhsT=dqc[n][i // 4][:, mine].bitcast(E5M2), lhsT_scale=dqs[n][i // 4][:, mine],
-                                        rhs=code[other][h][:, cols].bitcast(E4M3), rhs_scale=scale[other][h][:, cols], start=(g == 0), stop=(g == 1))
-
-            def take(eng):
-                out = outs.tile([P, 2, 256], F32, name="res", tag="res")
-                copy(eng, out[:].rearrange("p j c -> p (j c)"), o[:])
-                g, t = divmod(i, 4)
-                dst = out_0[g] if n == "a" else out_1[512 * g : 512 * (g + 1), :]
-                nc.sync.dma_start(out=dst.rearrange("(m t) d -> m t d", t=4)[:, t : t + 2, 512 * h + 256 * a : 512 * h + 256 * (a + 1)], in_=out[:])
-
-            return slot, take
-
         def halves(n, i, h, eng=A, paired=True):
             out = outs.tile([P, 2, 512], F32, name="res", tag="res")
             jobs = [product(n, i + j, h, out[:, j, :]) for j in range(2)]
             empty(eng, *(jobs if paired else reversed(jobs)))
-            g, t = divmod(i, 4)
-            dst = out_0[g] if n == "a" else out_1[512 * g : 512 * (g + 1), :]
-            nc.sync.dma_start(out=dst.rearrange("(m t) d -> m t d", t=4)[:, t : t + 2, 512 * h : 512 * (h + 1)], in_=out[:])
+            nc.sync.dma_start(out=rows_out(n, i, 2)[:, :, 512 * h : 512 * (h + 1)], in_=out[:])
+
+        def double(n, i, tag, eng=A):
+            out = keep.tile([P, 2, 1024], F32, name=f"double_{n}{i}", tag=tag, align_bytes=64)
+            for j in range(2):
+                empty(eng, *[product(n, i + j, h, out[:, j, 512 * h : 512 * (h + 1)]) for h in range(2)])
+            nc.sync.dma_start(out=rows_out(n, i, 2), in_=out[:])
 
         def whole(n, i, eng=A, other=None):
             if other is None:
@@ -255,9 +248,7 @@ def tile_localattention_pa_v_kernel(tc, x, Wq, bq, k, p, grad_out, out_0, out_1)
 
         def store(n, i, h=None):
             cols = slice(0, 1024) if h is None else slice(512 * h, 512 * (h + 1))
-            g, t = divmod(i, 4)
-            dst = out_0[g] if n == "a" else out_1[512 * g : 512 * (g + 1), :]
-            nc.sync.dma_start(out=dst.rearrange("(m t) d -> m t d", t=4)[:, t, cols], in_=res[n, i][:, cols])
+            nc.sync.dma_start(out=rows_out(n, i, 1)[:, 0, cols], in_=res[n, i][:, cols])
 
         make_identity(nc, ident[:])
         make_identity(nc, ident_bf[:])
@@ -278,7 +269,7 @@ def tile_localattention_pa_v_kernel(tc, x, Wq, bq, k, p, grad_out, out_0, out_1)
             row_sums(0, (2 * h, 2 * h + 1))
             soft(0, (2 * h, 2 * h + 1))
             empty(A, turn_dz(0, h))
-        weave_k(0, 0)
+        weave("k", 0, 0)
         for a in range(2):
             empty(A, weave_pe("k", 0, 1, a))
         quant("k", 0, 0, 2)
@@ -286,66 +277,64 @@ def tile_localattention_pa_v_kernel(tc, x, Wq, bq, k, p, grad_out, out_0, out_1)
         row_sums(1, range(4))
         soft(1, range(4))
         quant("k", 0, 2, 4)
-        empty(A, dqa(0, 0, 0), dqa(0, 1, 0))
-        empty(A, dqa(0, 2, 0), dqa(0, 3, 0))
+        empty(A, dh(0, 0, 0), dh(0, 1, 0))
+        empty(A, dh(0, 2, 0), dh(0, 3, 0))
         empty(A, turn_dz(1, 0), turn_dz(1, 1))
-        weave_k(1, 0)
-        weave_k(1, 1)
+        empty(A, dh(0, 0, 1), dh(0, 1, 1))
+        empty(A, dh(0, 2, 1), dh(0, 3, 1))
+        weave("k", 1, 0)
+        weave("k", 1, 1)
         quant_dz(1)
         quant("k", 1)
-        empty(A, dqa(0, 0, 1), dqa(0, 1, 1))
-        empty(A, dqa(0, 2, 1), dqa(0, 3, 1))
-        empty(A, dqb(0, 0), dqb(1, 0))
-        empty(A, dqb(2, 0), dqb(3, 0))
-        weave("w", 0, 0)
+        empty(V, weave_pe("w", 0, 0, 0), weave_pe("w", 0, 0, 1))
+        empty(A, turn_dq(0, 0), turn_dq(0, 1))
+        empty(A, turn_dq(0, 2), turn_dq(0, 3))
         weave("w", 1, 0)
-        quant_dq("a", 0, 4)
+        quant_a(0, 2)
         quant("w", 0)
+        quant_a(2, 4)
         for t in range(4):
-            empty(A, dqa(1, t, 0), dqa(1, t, 1))
-        early = [dqb(s, 1) for s in range(2)]
-        halves("a", 0, 0)
-        halves("a", 2, 0)
+            empty(A, dh(1, t, 0), dh(1, t, 1))
         weave("w", 0, 1)
-        quant_dq("a", 4, 6)
         weave("w", 1, 1)
-        quant_dq("a", 6, 8)
         quant("w", 1)
-        halves("a", 4, 0)
-        empty(A, *early)
-        halves("a", 6, 0)
         weave("x", 0, 0)
+        ahead = [product("a", t, 0) for t in range(2)]
+        empty(A, turn_dq(1, 0), turn_dq(1, 1))
+        ahead.append(product("a", 2, 0))
+        empty(A, ahead[0])
+        empty(A, turn_dq(1, 2), turn_dq(1, 3))
+        ahead.append(product("a", 3, 0))
+        quant_a(4, 6)
         weave("x", 1, 0)
-        weave("x", 0, 1)
+        quant_a(6, 8)
+        empty(A, product("a", 0, 1))
+        store("a", 0)
+        for t in range(1, 4):
+            empty(A, product("a", t, 1), ahead[t])
+            store("a", t)
+        weave_dq(0)
         quant("x", 0)
-        halves("a", 0, 1)
-        halves("a", 2, 1)
-        empty(A, dqb(2, 1), dqb(3, 1))
-        halves("a", 4, 1)
-        halves("a", 6, 1)
-        late = {4: [dqb(4, b) for b in range(2)]}
-        quant_dq("b", 0, 2)
+        weave("x", 0, 1)
+        quant_b(0)
+        weave_dq(1)
         weave("x", 1, 1)
-        quant_dq("b", 2, 4)
+        quant_b(1)
         quant("x", 1)
-        halves("b", 0, 0)
-        late[5] = [dqb(5, b) for b in range(2)]
-        halves("b", 2, 0, A, False)
-        empty(V, *late[4])
-        halves("b", 0, 1, A, False)
-        empty(V, *late[5])
-        quant_dq("b", 4, 5)
-        late[6] = [dqb(6, b) for b in range(2)]
-        halves("b", 2, 1, A, False)
-        empty(V, *late[6])
-        quant_dq("b", 5, 6)
-        late[7] = [dqb(7, b) for b in range(2)]
-        whole("b", 4, A, A)
-        empty(V, *late[7])
-        quant_dq("b", 6, 7)
-        whole("b", 5, A, A)
-        quant_dq("b", 7, 8)
-        whole("b", 6, A, V)
+        for t in range(4, 8):
+            whole("a", t)
+        weave_dq(2)
+        for s in range(2, 8):
+            if s < 7:
+                weave_dq(s + 1)
+            quant_b(s)
+        empty(A, product("b", 0, 0))
+        empty(A, product("b", 1, 0))
+        for s in range(2):
+            empty(A, product("b", s, 1))
+            store("b", s)
+        for s in range(2, 7):
+            whole("b", s, A, A if s < 4 else V)
         for h in range(2):
             empty((A, V)[h], product("b", 7, h))
             store("b", 7, h)

@@ -11,6 +11,7 @@ WIN = 152
 WIN_STEP = 120
 WIN_PITCH = 160
 GRP_BUFS = 3
+ROOM = {"a": ("raw_k1", "raw_w0", "raw_w1", "room0"), "b": ("room1", "room2", "raw_x0", "raw_x1")}
 
 F32 = mybir.dt.float32
 BF16 = mybir.dt.bfloat16
@@ -31,7 +32,7 @@ def tile_localattention_pa_v_kernel(tc, x, Wq, bq, k, p, grad_out, out_0, out_1)
     nc = tc.nc
     with ExitStack() as ctx:
         keep = ctx.enter_context(tc.tile_pool(name="keep", bufs=1))
-        outs = ctx.enter_context(tc.tile_pool(name="outs", bufs=10))
+        outs = ctx.enter_context(tc.tile_pool(name="outs", bufs=2))
         psum = ctx.enter_context(tc.psum_pool(name="psum", bufs=1))
         ctx.enter_context(tc.manual_schedule())
 
@@ -193,8 +194,9 @@ def tile_localattention_pa_v_kernel(tc, x, Wq, bq, k, p, grad_out, out_0, out_1)
 
         def weave_dq(s):
             dqw[s] = keep.tile([P, 1024], BF16, name=f"dqw{s}", tag="dqw", bufs=4, align_bytes=64)
-            src = dqn[:].rearrange("p (b t r w e) -> p r e b t w", b=2, t=4, r=4, e=2)[:, s // 2, s % 2]
-            nc.vector.tensor_copy(out=dqw[s][:].rearrange("p (b n i t) -> p b n t i", b=2, i=4, t=4), in_=src.rearrange("p b t (n i) -> p b n t i", i=4))
+            for b in range(B):
+                src = dqn[:].rearrange("p (b t g u w e) -> p b g u w t e", b=2, t=4, g=2, u=2, e=2)[:, b, s // 4, :, 32 * (s % 4) : 32 * (s % 4 + 1)]
+                nc.vector.tensor_copy(out=dqw[s][:, 512 * b : 512 * (b + 1)].rearrange("p (w u e t) -> p u w t e", u=2, e=2, t=4), in_=src)
 
         def quant_b(s):
             cols = slice(256 * (s % 4), 256 * (s % 4 + 1))
@@ -205,8 +207,9 @@ def tile_localattention_pa_v_kernel(tc, x, Wq, bq, k, p, grad_out, out_0, out_1)
             return slice(at, at + P)
 
         def rows_out(n, i, count):
-            rows = out_0[i // 4] if n == "a" else out_1[512 * (i // 4) : 512 * (i // 4 + 1), :]
-            return rows.rearrange("(m t) d -> m t d", t=4)[:, i % 4 : i % 4 + count, :]
+            if n == "a":
+                return out_0[i // 4].rearrange("(m t) d -> m t d", t=4)[:, i % 4 : i % 4 + count, :]
+            return out_1.rearrange("(s m) d -> m s d", m=P)[:, i : i + count, :]
 
         def product(n, i, h, dst=None):
             other = {"a": "w", "b": "x"}[n]
@@ -220,23 +223,15 @@ def tile_localattention_pa_v_kernel(tc, x, Wq, bq, k, p, grad_out, out_0, out_1)
             def take(eng):
                 if dst is not None:
                     return copy(eng, dst, o[:])
-                if (n, i) not in res:
-                    res[n, i] = outs.tile([P, 1024], F32, name="res", tag="res")
-                copy(eng, res[n, i][:, 512 * h : 512 * (h + 1)], o[:])
+                if (n, i // 2) not in res:
+                    res[n, i // 2] = keep.tile([P, 2, 1024], F32, name=f"res_{n}{i // 2}", tag=ROOM[n][i // 2], align_bytes=64)
+                copy(eng, res[n, i // 2][:, i % 2, 512 * h : 512 * (h + 1)], o[:])
 
             return slot, take
 
-        def halves(n, i, h, eng=A, paired=True):
-            out = outs.tile([P, 2, 512], F32, name="res", tag="res")
-            jobs = [product(n, i + j, h, out[:, j, :]) for j in range(2)]
-            empty(eng, *(jobs if paired else reversed(jobs)))
-            nc.sync.dma_start(out=rows_out(n, i, 2)[:, :, 512 * h : 512 * (h + 1)], in_=out[:])
-
-        def double(n, i, tag, eng=A):
-            out = keep.tile([P, 2, 1024], F32, name=f"double_{n}{i}", tag=tag, align_bytes=64)
-            for j in range(2):
-                empty(eng, *[product(n, i + j, h, out[:, j, 512 * h : 512 * (h + 1)]) for h in range(2)])
-            nc.sync.dma_start(out=rows_out(n, i, 2), in_=out[:])
+        def halves(n, i, h, eng=A):
+            empty(eng, product(n, i, h), product(n, i + 1, h))
+            store(n, i, 2, h)
 
         def whole(n, i, eng=A, other=None):
             if other is None:
@@ -244,11 +239,10 @@ def tile_localattention_pa_v_kernel(tc, x, Wq, bq, k, p, grad_out, out_0, out_1)
             else:
                 empty(eng, product(n, i, 0))
                 empty(other, product(n, i, 1))
-            store(n, i)
 
-        def store(n, i, h=None):
+        def store(n, i, count=1, h=None):
             cols = slice(0, 1024) if h is None else slice(512 * h, 512 * (h + 1))
-            nc.sync.dma_start(out=rows_out(n, i, 1)[:, 0, cols], in_=res[n, i][:, cols])
+            nc.sync.dma_start(out=rows_out(n, i, count)[:, :, cols], in_=res[n, i // 2][:, i % 2 : i % 2 + count, cols])
 
         make_identity(nc, ident[:])
         make_identity(nc, ident_bf[:])
@@ -292,49 +286,50 @@ def tile_localattention_pa_v_kernel(tc, x, Wq, bq, k, p, grad_out, out_0, out_1)
         weave("w", 1, 0)
         quant_a(0, 2)
         quant("w", 0)
-        quant_a(2, 4)
         for t in range(4):
             empty(A, dh(1, t, 0), dh(1, t, 1))
         weave("w", 0, 1)
         weave("w", 1, 1)
+        quant_a(2, 4)
         quant("w", 1)
-        weave("x", 0, 0)
-        ahead = [product("a", t, 0) for t in range(2)]
+        empty(A, product("a", 0, 0), product("a", 1, 0))
         empty(A, turn_dq(1, 0), turn_dq(1, 1))
-        ahead.append(product("a", 2, 0))
-        empty(A, ahead[0])
-        empty(A, turn_dq(1, 2), turn_dq(1, 3))
-        ahead.append(product("a", 3, 0))
+        turned = [turn_dq(1, 2), turn_dq(1, 3)]
+        ahead = product("a", 2, 0)
+        weave("x", 0, 0)
         quant_a(4, 6)
         weave("x", 1, 0)
-        quant_a(6, 8)
-        empty(A, product("a", 0, 1))
-        store("a", 0)
-        for t in range(1, 4):
-            empty(A, product("a", t, 1), ahead[t])
+        for t in range(2):
+            empty(A, product("a", t, 1))
             store("a", t)
+        empty(A, product("a", 2, 1), ahead)
+        store("a", 2)
+        empty(A, turned[0])
+        whole("a", 3)
+        store("a", 3)
+        empty(A, turned[1])
         weave_dq(0)
         quant("x", 0)
+        quant_a(6, 7)
         weave("x", 0, 1)
-        quant_b(0)
+        quant_a(7, 8)
         weave_dq(1)
+        quant_b(0)
         weave("x", 1, 1)
         quant_b(1)
         quant("x", 1)
         for t in range(4, 8):
             whole("a", t)
+            store("a", t)
         weave_dq(2)
         for s in range(2, 8):
             if s < 7:
                 weave_dq(s + 1)
             quant_b(s)
-        empty(A, product("b", 0, 0))
-        empty(A, product("b", 1, 0))
+        empty(A, product("b", 0, 0), product("b", 1, 0))
         for s in range(2):
             empty(A, product("b", s, 1))
             store("b", s)
-        for s in range(2, 7):
-            whole("b", s, A, A if s < 4 else V)
-        for h in range(2):
-            empty((A, V)[h], product("b", 7, h))
-            store("b", 7, h)
+        for s in range(2, 8):
+            whole("b", s, A, V if s >= 4 else None)
+            store("b", s)

@@ -280,15 +280,16 @@ def tile_localattention_pa_v_kernel(tc, x, Wq, bq, k, p, grad_out, out_0, out_1)
         weave("k", 1, 1)
         quant_dz(1)
         quant("k", 1)
-        empty(V, weave_pe("w", 0, 0, 0), weave_pe("w", 0, 0, 1))
+        woven_w = [weave_pe("w", 0, 0, a) for a in range(2)]
         empty(A, turn_dq(0, 0), turn_dq(0, 1))
+        empty(A, *woven_w)
         empty(A, turn_dq(0, 2), turn_dq(0, 3))
         weave("w", 1, 0)
+        weave("w", 0, 1)
         quant_a(0, 2)
         quant("w", 0)
         for t in range(4):
             empty(A, dh(1, t, 0), dh(1, t, 1))
-        weave("w", 0, 1)
         weave("w", 1, 1)
         quant_a(2, 4)
         quant("w", 1)
@@ -297,27 +298,27 @@ def tile_localattention_pa_v_kernel(tc, x, Wq, bq, k, p, grad_out, out_0, out_1)
         turned = [turn_dq(1, 2), turn_dq(1, 3)]
         ahead = product("a", 2, 0)
         weave("x", 0, 0)
-        quant_a(4, 6)
         weave("x", 1, 0)
+        weave_dq(0)
+        quant("x", 0)
+        quant_a(4, 6)
+        weave("x", 0, 1)
+        quant_b(0)
         for t in range(2):
             empty(A, product("a", t, 1))
             store("a", t)
         empty(A, product("a", 2, 1), ahead)
         store("a", 2)
         empty(A, turned[0])
+        quant_a(6, 7)
+        weave("x", 1, 1)
         whole("a", 3)
         store("a", 3)
         empty(A, turned[1])
-        weave_dq(0)
-        quant("x", 0)
-        quant_a(6, 7)
-        weave("x", 0, 1)
         quant_a(7, 8)
         weave_dq(1)
-        quant_b(0)
-        weave("x", 1, 1)
-        quant_b(1)
         quant("x", 1)
+        quant_b(1)
         for t in range(4, 8):
             whole("a", t)
             store("a", t)
@@ -326,10 +327,6 @@ def tile_localattention_pa_v_kernel(tc, x, Wq, bq, k, p, grad_out, out_0, out_1)
             if s < 7:
                 weave_dq(s + 1)
             quant_b(s)
-        empty(A, product("b", 0, 0), product("b", 1, 0))
-        for s in range(2):
-            empty(A, product("b", s, 1))
-            store("b", s)
-        for s in range(2, 8):
+        for s in range(8):
             whole("b", s, A, V if s >= 4 else None)
             store("b", s)

@@ -11,6 +11,7 @@ WIN = 152
 WIN_STEP = 120
 WIN_PITCH = 160
 GRP_BUFS = 3
+RUN = 4
 ROOM = {"a": ("raw_k1", "raw_w0", "raw_w1", "room0"), "b": ("room1", "room2", "raw_x0", "raw_x1")}
 
 F32 = mybir.dt.float32
@@ -143,17 +144,23 @@ def tile_localattention_pa_v_kernel(tc, x, Wq, bq, k, p, grad_out, out_0, out_1)
             o, i = home(n, b, h)
             return grouped(n, o)[:, 2048 * i : 2048 * (i + 1)]
 
+        def places(n, rows, walk):
+            j = "(e u)" if n == "w" else "(u e)"
+            if "i" in walk:
+                return rows.rearrange("p %s (c i) -> p %s" % (j, walk), u=2, i=RUN)
+            return rows.rearrange("p %s c -> p %s" % (j, walk), u=2)
+
         def weave_pe(n, b, h, a):
             slot, t = bank(BF16, 1024)
             for c in range(2):
                 cols = slice(256 * a + P * c, 256 * a + P * (c + 1))
-                nc.tensor.matmul(t[:, 512 * c : 512 * (c + 1)], lhsT=ident_bf[:], rhs=raw[n, b, h][:, :, cols].rearrange("p j c -> p c j"), start=True, stop=True)
+                nc.tensor.matmul(t[:, 512 * c : 512 * (c + 1)], lhsT=ident_bf[:], rhs=places(n, raw[n, b, h][:, :, cols], "c u e"), start=True, stop=True)
             dst = woven(n, b, h)[:, 1024 * a : 1024 * (a + 1)]
             return slot, lambda eng: copy(eng, dst, t[:])
 
         def weave(n, b, h, a0=0, a1=2, eng=V):
-            dst = woven(n, b, h)[:, 1024 * a0 : 1024 * a1].rearrange("p (c i t) -> p c t i", i=4, t=4)
-            copy(eng, dst, raw[n, b, h][:, :, 256 * a0 : 256 * a1].rearrange("p t (c i) -> p c t i", i=4))
+            dst = woven(n, b, h)[:, 1024 * a0 : 1024 * a1].rearrange("p (c i u e) -> p c u e i", i=RUN, u=2, e=2)
+            copy(eng, dst, places(n, raw[n, b, h][:, :, 256 * a0 : 256 * a1], "c u e i"))
 
         def quant(n, o, c0=0, c1=4):
             cols = slice(256 * c0, 256 * c1)
@@ -166,8 +173,8 @@ def tile_localattention_pa_v_kernel(tc, x, Wq, bq, k, p, grad_out, out_0, out_1)
                                 rhs=code["k"][b][:, cols].bitcast(E4M3), rhs_scale=scale["k"][b][:, cols], start=True, stop=True)
             at = 4096 * b + 1024 * t + 512 * h
 
-            dst = dqn[:, at : at + 512].rearrange("p (u w e) -> p u w e", u=2, e=2)
-            src = o[:].rearrange("p (w u e) -> p u w e", u=2, e=2)
+            dst = dqn[:, at : at + 512].rearrange("p (u m) -> p u m", u=2)
+            src = o[:].rearrange("p (m u) -> p u m", u=2)
 
             def take(eng):
                 if eng == A:
@@ -194,9 +201,8 @@ def tile_localattention_pa_v_kernel(tc, x, Wq, bq, k, p, grad_out, out_0, out_1)
 
         def weave_dq(s):
             dqw[s] = keep.tile([P, 1024], BF16, name=f"dqw{s}", tag="dqw", bufs=4, align_bytes=64)
-            for b in range(B):
-                src = dqn[:].rearrange("p (b t g u w e) -> p b g u w t e", b=2, t=4, g=2, u=2, e=2)[:, b, s // 4, :, 32 * (s % 4) : 32 * (s % 4 + 1)]
-                nc.vector.tensor_copy(out=dqw[s][:, 512 * b : 512 * (b + 1)].rearrange("p (w u e t) -> p u w t e", u=2, e=2, t=4), in_=src)
+            src = dqn[:].rearrange("p (b t s c i) -> p s b c t i", b=2, t=4, s=8, i=RUN)[:, s]
+            nc.vector.tensor_copy(out=dqw[s][:].rearrange("p (b c i t) -> p b c t i", b=2, i=RUN, t=4), in_=src)
 
         def quant_b(s):
             cols = slice(256 * (s % 4), 256 * (s % 4 + 1))
@@ -209,7 +215,7 @@ def tile_localattention_pa_v_kernel(tc, x, Wq, bq, k, p, grad_out, out_0, out_1)
         def rows_out(n, i, count):
             if n == "a":
                 return out_0[i // 4].rearrange("(m t) d -> m t d", t=4)[:, i % 4 : i % 4 + count, :]
-            return out_1.rearrange("(s m) d -> m s d", m=P)[:, i : i + count, :]
+            return out_1.rearrange("(g q m u) d -> g u m q d", g=2, q=2, u=2)[i // 4, i // 2 % 2][:, i % 2 : i % 2 + count, :]
 
         def product(n, i, h, dst=None):
             other = {"a": "w", "b": "x"}[n]
@@ -288,42 +294,45 @@ def tile_localattention_pa_v_kernel(tc, x, Wq, bq, k, p, grad_out, out_0, out_1)
         weave("w", 0, 1)
         quant_a(0, 2)
         quant("w", 0)
-        for t in range(4):
-            empty(A, dh(1, t, 0), dh(1, t, 1))
+        held = [dh(1, t, h) for t in range(4) for h in range(2)]
         weave("w", 1, 1)
         quant_a(2, 4)
         quant("w", 1)
-        empty(A, product("a", 0, 0), product("a", 1, 0))
-        empty(A, turn_dq(1, 0), turn_dq(1, 1))
-        turned = [turn_dq(1, 2), turn_dq(1, 3)]
-        ahead = product("a", 2, 0)
-        weave("x", 0, 0)
-        weave("x", 1, 0)
-        weave_dq(0)
-        quant("x", 0)
-        quant_a(4, 6)
-        weave("x", 0, 1)
-        quant_b(0)
-        for t in range(2):
-            empty(A, product("a", t, 1))
-            store("a", t)
-        empty(A, product("a", 2, 1), ahead)
+        empty(A, *held[0:2])
+        first = [product("a", t, 0) for t in range(2)]
+        empty(A, *held[2:4])
+        turned = [turn_dq(1, t) for t in range(2)]
+        empty(A, *held[4:6])
+        second = [product("a", t, 1) for t in range(2)]
+        empty(A, *held[6:8])
+        late = [turn_dq(1, t) for t in range(2, 4)]
+        empty(A, *turned)
+        empty(A, second[0], first[0])
+        store("a", 0)
+        empty(A, first[1], second[1])
+        store("a", 1)
+        third = [product("a", 2, h) for h in range(2)]
+        empty(A, late[0])
+        empty(A, *third)
         store("a", 2)
-        empty(A, turned[0])
-        quant_a(6, 7)
-        weave("x", 1, 1)
+        empty(A, late[1])
         whole("a", 3)
         store("a", 3)
-        empty(A, turned[1])
-        quant_a(7, 8)
-        weave_dq(1)
+        weave("x", 0, 0)
+        weave("x", 1, 0)
+        quant_a(4, 6)
+        weave("x", 0, 1)
+        quant("x", 0)
+        weave("x", 1, 1)
+        quant_a(6, 8)
+        weave_dq(0)
         quant("x", 1)
-        quant_b(1)
+        quant_b(0)
         for t in range(4, 8):
             whole("a", t)
             store("a", t)
-        weave_dq(2)
-        for s in range(2, 8):
+        weave_dq(1)
+        for s in range(1, 8):
             if s < 7:
                 weave_dq(s + 1)
             quant_b(s)

@@ -111,7 +111,7 @@ def tile_localattention_pa_v_kernel(tc, x, Wq, bq, k, p, grad_out, out_0, out_1)
             raw[n, b, h] = t[:]
 
         def band(i):
-            lo, hi = max(P * i - 8, 0), min(P * i + 136, S)
+            lo, hi = max(P * i - HALF - 1, 0), min(P * (i + 1) + HALF + 1, S)
             return slice(lo, hi), slice(lo - WIN_STEP * i, hi - WIN_STEP * i)
 
         def row_sums(b, tiles_):
@@ -122,7 +122,9 @@ def tile_localattention_pa_v_kernel(tc, x, Wq, bq, k, p, grad_out, out_0, out_1)
         def soft(b, tiles_):
             for i in tiles_:
                 cols, w = band(i)
-                nc.vector.scalar_tensor_tensor(out=dz[b][i][:, cols], in0=gw[b][:, i, w], scalar=rsum[b][:, i : i + 1], in1=pw[b][:, i, w], op0=SUB, op1=MULT)
+                dst = dz[b][i][:].rearrange("p (u m) -> p u m", u=2)[:, :, cols.start // 2 : cols.stop // 2]
+                g, q = (src[b][:, i, w].rearrange("p (m u) -> p u m", u=2) for src in (gw, pw))
+                nc.vector.scalar_tensor_tensor(out=dst, in0=g, scalar=rsum[b][:, i : i + 1], in1=q, op0=SUB, op1=MULT)
 
         def turn_dz(b, h):
             n, t = bank()
@@ -130,7 +132,7 @@ def tile_localattention_pa_v_kernel(tc, x, Wq, bq, k, p, grad_out, out_0, out_1)
                 words = dz[b][2 * h + i][:].bitcast(F32)
                 for u in range(2):
                     at = 256 * u + 128 * i
-                    nc.tensor.transpose(t[:, at : at + 128], words[:, u : S // 2 : 2], ident[:])
+                    nc.tensor.transpose(t[:, at : at + 128], words[:, P * u : P * (u + 1)], ident[:])
             words = dzg[b][:].bitcast(F32).rearrange("p (t m u) -> p t m u", t=4, u=2)
             return n, lambda eng: copy(eng, words[:, :, 64 * h : 64 * (h + 1), :], t[:].rearrange("p (u m t) -> p t m u", u=2, t=4))
 
@@ -145,7 +147,7 @@ def tile_localattention_pa_v_kernel(tc, x, Wq, bq, k, p, grad_out, out_0, out_1)
             return grouped(n, o)[:, 2048 * i : 2048 * (i + 1)]
 
         def places(n, rows, walk):
-            j = "(e u)" if n == "w" else "(u e)"
+            j = "(u e)" if n == "x" else "(e u)"
             if "i" in walk:
                 return rows.rearrange("p %s (c i) -> p %s" % (j, walk), u=2, i=RUN)
             return rows.rearrange("p %s c -> p %s" % (j, walk), u=2)
@@ -251,10 +253,10 @@ def tile_localattention_pa_v_kernel(tc, x, Wq, bq, k, p, grad_out, out_0, out_1)
             nc.sync.dma_start(out=rows_out(n, i, count)[:, :, cols], in_=res[n, i // 2][:, i % 2 : i % 2 + count, cols])
 
         make_identity(nc, ident[:])
-        make_identity(nc, ident_bf[:])
         for b in range(B):
             for i in range(4):
                 nc.vector.memset(dz[b][i][:].bitcast(F32), 0.0)
+        nc.vector.tensor_copy(out=ident_bf[:], in_=ident[:])
         load_window(0, 0, 2)
         load_window(0, 2, 4)
         load_half("k", 0, 0)
@@ -270,14 +272,15 @@ def tile_localattention_pa_v_kernel(tc, x, Wq, bq, k, p, grad_out, out_0, out_1)
             soft(0, (2 * h, 2 * h + 1))
             empty(A, turn_dz(0, h))
         weave("k", 0, 0)
-        for a in range(2):
-            empty(A, weave_pe("k", 0, 1, a))
+        weave("k", 0, 1, 0, 1, A)
+        empty(A, weave_pe("k", 0, 1, 1))
         quant("k", 0, 0, 2)
         quant_dz(0)
         row_sums(1, range(4))
         soft(1, range(4))
         quant("k", 0, 2, 4)
-        empty(A, dh(0, 0, 0), dh(0, 1, 0))
+        empty(A, dh(0, 0, 0))
+        empty(A, dh(0, 1, 0))
         empty(A, dh(0, 2, 0), dh(0, 3, 0))
         empty(A, turn_dz(1, 0), turn_dz(1, 1))
         empty(A, dh(0, 0, 1), dh(0, 1, 1))
@@ -290,8 +293,8 @@ def tile_localattention_pa_v_kernel(tc, x, Wq, bq, k, p, grad_out, out_0, out_1)
         empty(A, turn_dq(0, 0), turn_dq(0, 1))
         empty(A, *woven_w)
         empty(A, turn_dq(0, 2), turn_dq(0, 3))
-        weave("w", 1, 0)
         weave("w", 0, 1)
+        weave("w", 1, 0)
         quant_a(0, 2)
         quant("w", 0)
         held = [dh(1, t, h) for t in range(4) for h in range(2)]

@@ -256,7 +256,6 @@ def tile_localattention_pa_v_kernel(tc, x, Wq, bq, k, p, grad_out, out_0, out_1)
         for b in range(B):
             for i in range(4):
                 nc.vector.memset(dz[b][i][:].bitcast(F32), 0.0)
-        nc.vector.tensor_copy(out=ident_bf[:], in_=ident[:])
         load_window(0, 0, 2)
         load_window(0, 2, 4)
         load_half("k", 0, 0)
@@ -272,23 +271,23 @@ def tile_localattention_pa_v_kernel(tc, x, Wq, bq, k, p, grad_out, out_0, out_1)
             soft(0, (2 * h, 2 * h + 1))
             empty(A, turn_dz(0, h))
         weave("k", 0, 0)
-        weave("k", 0, 1, 0, 1, A)
-        empty(A, weave_pe("k", 0, 1, 1))
+        nc.vector.tensor_copy(out=ident_bf[:], in_=ident[:])
+        weave("k", 0, 1, eng=A)
         quant("k", 0, 0, 2)
         quant_dz(0)
         row_sums(1, range(4))
         soft(1, range(4))
         quant("k", 0, 2, 4)
-        empty(A, dh(0, 0, 0))
-        empty(A, dh(0, 1, 0))
-        empty(A, dh(0, 2, 0), dh(0, 3, 0))
+        for t in range(4):
+            empty(A, dh(0, t, 0))
         empty(A, turn_dz(1, 0), turn_dz(1, 1))
         empty(A, dh(0, 0, 1), dh(0, 1, 1))
         empty(A, dh(0, 2, 1), dh(0, 3, 1))
         weave("k", 1, 0)
         weave("k", 1, 1)
+        quant("k", 1, 0, 2)
         quant_dz(1)
-        quant("k", 1)
+        quant("k", 1, 2, 4)
         woven_w = [weave_pe("w", 0, 0, a) for a in range(2)]
         empty(A, turn_dq(0, 0), turn_dq(0, 1))
         empty(A, *woven_w)

@@ -41,7 +41,6 @@ def tile_localattention_pa_v_kernel(tc, x, Wq, bq, k, p, grad_out, out_0, out_1)
             return [keep.tile(shape, dtype, name=f"{name}{i}", tag=f"{name}{i}", align_bytes=64) for i in range(n)]
 
         ident = keep.tile([P, P], F32, name="ident", tag="ident", align_bytes=64)
-        ident_bf = keep.tile([P, P], BF16, name="ident_bf", tag="ident_bf", align_bytes=64)
         pw = tiles("pw", [P, 4, WIN_PITCH], F32)
         gw = tiles("gw", [P, 4, WIN_PITCH], BF16)
         prod = keep.tile([P, 4, WIN_PITCH], F32, name="prod", tag="prod", align_bytes=64)
@@ -146,23 +145,13 @@ def tile_localattention_pa_v_kernel(tc, x, Wq, bq, k, p, grad_out, out_0, out_1)
             o, i = home(n, b, h)
             return grouped(n, o)[:, 2048 * i : 2048 * (i + 1)]
 
-        def places(n, rows, walk):
+        def places(n, rows):
             j = "(u e)" if n == "x" else "(e u)"
-            if "i" in walk:
-                return rows.rearrange("p %s (c i) -> p %s" % (j, walk), u=2, i=RUN)
-            return rows.rearrange("p %s c -> p %s" % (j, walk), u=2)
+            return rows.rearrange("p %s (c i) -> p c u e i" % j, u=2, i=RUN)
 
-        def weave_pe(n, b, h, a):
-            slot, t = bank(BF16, 1024)
-            for c in range(2):
-                cols = slice(256 * a + P * c, 256 * a + P * (c + 1))
-                nc.tensor.matmul(t[:, 512 * c : 512 * (c + 1)], lhsT=ident_bf[:], rhs=places(n, raw[n, b, h][:, :, cols], "c u e"), start=True, stop=True)
-            dst = woven(n, b, h)[:, 1024 * a : 1024 * (a + 1)]
-            return slot, lambda eng: copy(eng, dst, t[:])
-
-        def weave(n, b, h, a0=0, a1=2, eng=V):
-            dst = woven(n, b, h)[:, 1024 * a0 : 1024 * a1].rearrange("p (c i u e) -> p c u e i", i=RUN, u=2, e=2)
-            copy(eng, dst, places(n, raw[n, b, h][:, :, 256 * a0 : 256 * a1], "c u e i"))
+        def weave(n, b, h, c0=0, c1=512, eng=V):
+            dst = woven(n, b, h)[:, 4 * c0 : 4 * c1].rearrange("p (c i u e) -> p c u e i", i=RUN, u=2, e=2)
+            copy(eng, dst, places(n, raw[n, b, h][:, :, c0:c1]))
 
         def quant(n, o, c0=0, c1=4):
             cols = slice(256 * c0, 256 * c1)
@@ -271,7 +260,6 @@ def tile_localattention_pa_v_kernel(tc, x, Wq, bq, k, p, grad_out, out_0, out_1)
             soft(0, (2 * h, 2 * h + 1))
             empty(A, turn_dz(0, h))
         weave("k", 0, 0)
-        nc.vector.tensor_copy(out=ident_bf[:], in_=ident[:])
         weave("k", 0, 1, eng=A)
         quant("k", 0, 0, 2)
         quant_dz(0)
@@ -288,10 +276,10 @@ def tile_localattention_pa_v_kernel(tc, x, Wq, bq, k, p, grad_out, out_0, out_1)
         quant("k", 1, 0, 2)
         quant_dz(1)
         quant("k", 1, 2, 4)
-        woven_w = [weave_pe("w", 0, 0, a) for a in range(2)]
         empty(A, turn_dq(0, 0), turn_dq(0, 1))
-        empty(A, *woven_w)
+        weave("w", 0, 0, 0, 192, A)
         empty(A, turn_dq(0, 2), turn_dq(0, 3))
+        weave("w", 0, 0, 192, 512)
         weave("w", 0, 1)
         weave("w", 1, 0)
         quant_a(0, 2)

@@ -1,7 +1,6 @@
 from contextlib import ExitStack
 
 import concourse.mybir as mybir
-from concourse.masks import make_identity
 
 B, S, D, E = 2, 512, 1024, 1024
 HALF = 5
@@ -17,11 +16,13 @@ ROOM = {"a": ("raw_k1", "raw_w0", "raw_w1", "room0"), "b": ("room1", "room2", "r
 F32 = mybir.dt.float32
 BF16 = mybir.dt.bfloat16
 U32 = mybir.dt.uint32
+I32 = mybir.dt.int32
 U8 = mybir.dt.uint8
 E4M3 = mybir.dt.float8_e4m3fn_x4
 E5M2 = mybir.dt.float8_e5m2_x4
 MULT = mybir.AluOpType.mult
 SUB = mybir.AluOpType.subtract
+EQUAL = mybir.AluOpType.is_equal
 COPY = mybir.ActivationFunctionType.Copy
 
 FLOPS = 2 * B * S * S * E + 4 * T * E * D
@@ -41,6 +42,7 @@ def tile_localattention_pa_v_kernel(tc, x, Wq, bq, k, p, grad_out, out_0, out_1)
             return [keep.tile(shape, dtype, name=f"{name}{i}", tag=f"{name}{i}", align_bytes=64) for i in range(n)]
 
         ident = keep.tile([P, P], F32, name="ident", tag="ident", align_bytes=64)
+        apart = keep.tile([P, P], I32, name="apart", tag="apart", align_bytes=64)
         pw = tiles("pw", [P, 4, WIN_PITCH], F32)
         gw = tiles("gw", [P, 4, WIN_PITCH], BF16)
         prod = keep.tile([P, 4, WIN_PITCH], F32, name="prod", tag="prod", align_bytes=64)
@@ -112,6 +114,10 @@ def tile_localattention_pa_v_kernel(tc, x, Wq, bq, k, p, grad_out, out_0, out_1)
         def band(i):
             lo, hi = max(P * i - HALF - 1, 0), min(P * (i + 1) + HALF + 1, S)
             return slice(lo, hi), slice(lo - WIN_STEP * i, hi - WIN_STEP * i)
+
+        def clear(b, tiles_):
+            for i in tiles_:
+                nc.vector.memset(dz[b][i][:].bitcast(F32), 0.0)
 
         def row_sums(b, tiles_):
             for i in tiles_:
@@ -241,10 +247,9 @@ def tile_localattention_pa_v_kernel(tc, x, Wq, bq, k, p, grad_out, out_0, out_1)
             cols = slice(0, 1024) if h is None else slice(512 * h, 512 * (h + 1))
             nc.sync.dma_start(out=rows_out(n, i, count)[:, :, cols], in_=res[n, i // 2][:, i % 2 : i % 2 + count, cols])
 
-        make_identity(nc, ident[:])
-        for b in range(B):
-            for i in range(4):
-                nc.vector.memset(dz[b][i][:].bitcast(F32), 0.0)
+        nc.gpsimd.iota(apart[:], pattern=[[-1, P]], base=0, channel_multiplier=1)
+        clear(0, range(4))
+        nc.vector.tensor_scalar(out=ident[:], in0=apart[:], scalar1=0.0, scalar2=None, op0=EQUAL)
         load_window(0, 0, 2)
         load_window(0, 2, 4)
         load_half("k", 0, 0)
@@ -259,7 +264,9 @@ def tile_localattention_pa_v_kernel(tc, x, Wq, bq, k, p, grad_out, out_0, out_1)
             row_sums(0, (2 * h, 2 * h + 1))
             soft(0, (2 * h, 2 * h + 1))
             empty(A, turn_dz(0, h))
+        clear(1, (0, 1))
         weave("k", 0, 0)
+        clear(1, (2, 3))
         weave("k", 0, 1, eng=A)
         quant("k", 0, 0, 2)
         quant_dz(0)

@@ -6,8 +6,9 @@ B, S, D, E = 2, 512, 1024, 1024
 HALF = 5
 T = B * S
 P = 128
-WIN = 152
-WIN_STEP = 120
+WIN = 140
+WIN_STEP = 122
+WIN_PAIR = 250
 WIN_PITCH = 160
 GRP_BUFS = 3
 RUN = 4
@@ -34,7 +35,6 @@ def tile_localattention_pa_v_kernel(tc, x, Wq, bq, k, p, grad_out, out_0, out_1)
     nc = tc.nc
     with ExitStack() as ctx:
         keep = ctx.enter_context(tc.tile_pool(name="keep", bufs=1))
-        outs = ctx.enter_context(tc.tile_pool(name="outs", bufs=2))
         psum = ctx.enter_context(tc.psum_pool(name="psum", bufs=1))
         ctx.enter_context(tc.manual_schedule())
 
@@ -47,7 +47,7 @@ def tile_localattention_pa_v_kernel(tc, x, Wq, bq, k, p, grad_out, out_0, out_1)
         gw = tiles("gw", [P, 4, WIN_PITCH], BF16)
         prod = keep.tile([P, 4, WIN_PITCH], F32, name="prod", tag="prod", align_bytes=64)
         rsum = tiles("rsum", [P, 4], F32)
-        dz = [tiles(f"dz{b}_", [P, S], BF16, 4) for b in range(B)]
+        dz = keep.tile([P, 4 * S], BF16, name="dz", tag="dz", align_bytes=64)
         dzg = tiles("dzg", [P, 4 * S], BF16)
         dzc = tiles("dzc", [P, S], U32)
         dzs = tiles("dzs", [P, S], U8)
@@ -85,17 +85,19 @@ def tile_localattention_pa_v_kernel(tc, x, Wq, bq, k, p, grad_out, out_0, out_1)
                 job(eng)
             spare.extend(n for n, job in jobs)
 
-        def load_window(b, i0=0, i1=4):
+        def load_window(b, h):
             step = P * S + WIN_STEP
+            at = (b * S + 2 * P * h) * S + WIN_PAIR * h
             for dst, src in ((gw[b], grad_out), (pw[b], p)):
                 flat = src.rearrange("b s j -> (b s j)")
-                if b == 0:
-                    rows = flat[: 4 * step].rearrange("(i y) -> i y", i=4)[:, : P * S]
+                if h == 0:
+                    rows = flat[at : at + 2 * step].rearrange("(i y) -> i y", i=2)[:, : P * S]
                     win = rows.rearrange("i (r j) -> r i j", j=S)[:, :, :WIN]
                 else:
-                    rows = flat[B * S * S - 4 * step :].rearrange("(i y) -> i y", i=4)[:, WIN_STEP:]
+                    back = at - WIN_STEP - (S - WIN)
+                    rows = flat[back : back + 2 * step].rearrange("(i y) -> i y", i=2)[:, WIN_STEP:]
                     win = rows.rearrange("i (r j) -> r i j", j=S)[:, :, S - WIN :]
-                nc.sync.dma_start(out=dst[:, i0:i1, :WIN], in_=win[:, i0:i1, :])
+                nc.sync.dma_start(out=dst[:, 2 * h : 2 * h + 2, :WIN], in_=win)
 
         def rows_of(n, b):
             return {"k": lambda: k[b], "x": lambda: x[b], "w": lambda: Wq[512 * b : 512 * (b + 1), :]}[n]().rearrange("(p j) c -> p j c", j=4)
@@ -113,11 +115,8 @@ def tile_localattention_pa_v_kernel(tc, x, Wq, bq, k, p, grad_out, out_0, out_1)
 
         def band(i):
             lo, hi = max(P * i - HALF - 1, 0), min(P * (i + 1) + HALF + 1, S)
-            return slice(lo, hi), slice(lo - WIN_STEP * i, hi - WIN_STEP * i)
-
-        def clear(b, tiles_):
-            for i in tiles_:
-                nc.vector.memset(dz[b][i][:].bitcast(F32), 0.0)
+            at = WIN_PAIR * (i // 2) + WIN_STEP * (i % 2)
+            return slice(lo, hi), slice(lo - at, hi - at)
 
         def row_sums(b, tiles_):
             for i in tiles_:
@@ -127,22 +126,23 @@ def tile_localattention_pa_v_kernel(tc, x, Wq, bq, k, p, grad_out, out_0, out_1)
         def soft(b, tiles_):
             for i in tiles_:
                 cols, w = band(i)
-                dst = dz[b][i][:].rearrange("p (u m) -> p u m", u=2)[:, :, cols.start // 2 : cols.stop // 2]
+                dst = dz[:].rearrange("p (i u m) -> p i u m", i=4, u=2)[:, i, :, cols.start // 2 : cols.stop // 2]
                 g, q = (src[b][:, i, w].rearrange("p (m u) -> p u m", u=2) for src in (gw, pw))
                 nc.vector.scalar_tensor_tensor(out=dst, in0=g, scalar=rsum[b][:, i : i + 1], in1=q, op0=SUB, op1=MULT)
 
         def turn_dz(b, h):
             n, t = bank()
             for i in range(2):
-                words = dz[b][2 * h + i][:].bitcast(F32)
+                words = dz[:, S * (2 * h + i) : S * (2 * h + i + 1)].bitcast(F32)
                 for u in range(2):
                     at = 256 * u + 128 * i
                     nc.tensor.transpose(t[:, at : at + 128], words[:, P * u : P * (u + 1)], ident[:])
             words = dzg[b][:].bitcast(F32).rearrange("p (t m u) -> p t m u", t=4, u=2)
             return n, lambda eng: copy(eng, words[:, :, 64 * h : 64 * (h + 1), :], t[:].rearrange("p (u m t) -> p t m u", u=2, t=4))
 
-        def quant_dz(b):
-            nc.vector.quantize_mx(out=dzc[b][:].bitcast(E5M2), scales=dzs[b][:], in_=dzg[b][:])
+        def quant_dz(b, t0=0, t1=4):
+            cols = slice(P * t0, P * t1)
+            nc.vector.quantize_mx(out=dzc[b][:, cols].bitcast(E5M2), scales=dzs[b][:, cols], in_=dzg[b][:, S * t0 : S * t1])
 
         def home(n, b, h):
             return (b, h) if n == "k" else (h, b)
@@ -163,11 +163,13 @@ def tile_localattention_pa_v_kernel(tc, x, Wq, bq, k, p, grad_out, out_0, out_1)
             cols = slice(256 * c0, 256 * c1)
             nc.vector.quantize_mx(out=code[n][o][:, cols].bitcast(E4M3), scales=scale[n][o][:, cols], in_=grouped(n, o)[:, 1024 * c0 : 1024 * c1])
 
-        def dh(b, t, h):
+        def dh(b, t, h, width=512):
             n, o = bank()
-            rows, cols = slice(P * t, P * (t + 1)), slice(512 * h, 512 * (h + 1))
-            nc.tensor.matmul_mx(out=o[:], lhsT=dzc[b][:, rows].bitcast(E5M2), lhsT_scale=dzs[b][:, rows],
-                                rhs=code["k"][b][:, cols].bitcast(E4M3), rhs_scale=scale["k"][b][:, cols], start=True, stop=True)
+            rows = slice(P * t, P * (t + 1))
+            for c in range(0, 512, width):
+                cols = slice(512 * h + c, 512 * h + c + width)
+                nc.tensor.matmul_mx(out=o[:, c : c + width], lhsT=dzc[b][:, rows].bitcast(E5M2), lhsT_scale=dzs[b][:, rows],
+                                    rhs=code["k"][b][:, cols].bitcast(E4M3), rhs_scale=scale["k"][b][:, cols], start=True, stop=True)
             at = 4096 * b + 1024 * t + 512 * h
 
             dst = dqn[:, at : at + 512].rearrange("p (u m) -> p u m", u=2)
@@ -209,12 +211,12 @@ def tile_localattention_pa_v_kernel(tc, x, Wq, bq, k, p, grad_out, out_0, out_1)
             at = 256 * (i % 4) + P * g
             return slice(at, at + P)
 
-        def rows_out(n, i, count):
+        def rows_out(n, i):
             if n == "a":
-                return out_0[i // 4].rearrange("(m t) d -> m t d", t=4)[:, i % 4 : i % 4 + count, :]
-            return out_1.rearrange("(g q m u) d -> g u m q d", g=2, q=2, u=2)[i // 4, i // 2 % 2][:, i % 2 : i % 2 + count, :]
+                return out_0[i // 4].rearrange("(m t) d -> m t d", t=4)[:, i % 4, :]
+            return out_1.rearrange("(g q m u) d -> g u m q d", g=2, q=2, u=2)[i // 4, i // 2 % 2][:, i % 2, :]
 
-        def product(n, i, h, dst=None):
+        def product(n, i, h):
             other = {"a": "w", "b": "x"}[n]
             slot, o = bank()
             for g in range(2):
@@ -224,17 +226,11 @@ def tile_localattention_pa_v_kernel(tc, x, Wq, bq, k, p, grad_out, out_0, out_1)
                                     rhs=code[other][h][:, cols].bitcast(E4M3), rhs_scale=scale[other][h][:, cols], start=(g == 0), stop=(g == 1))
 
             def take(eng):
-                if dst is not None:
-                    return copy(eng, dst, o[:])
                 if (n, i // 2) not in res:
                     res[n, i // 2] = keep.tile([P, 2, 1024], F32, name=f"res_{n}{i // 2}", tag=ROOM[n][i // 2], align_bytes=64)
                 copy(eng, res[n, i // 2][:, i % 2, 512 * h : 512 * (h + 1)], o[:])
 
             return slot, take
-
-        def halves(n, i, h, eng=A):
-            empty(eng, product(n, i, h), product(n, i + 1, h))
-            store(n, i, 2, h)
 
         def whole(n, i, eng=A, other=None):
             if other is None:
@@ -243,18 +239,17 @@ def tile_localattention_pa_v_kernel(tc, x, Wq, bq, k, p, grad_out, out_0, out_1)
                 empty(eng, product(n, i, 0))
                 empty(other, product(n, i, 1))
 
-        def store(n, i, count=1, h=None):
-            cols = slice(0, 1024) if h is None else slice(512 * h, 512 * (h + 1))
-            nc.sync.dma_start(out=rows_out(n, i, count)[:, :, cols], in_=res[n, i // 2][:, i % 2 : i % 2 + count, cols])
+        def store(n, i):
+            nc.sync.dma_start(out=rows_out(n, i), in_=res[n, i // 2][:, i % 2, :])
 
         nc.gpsimd.iota(apart[:], pattern=[[-1, P]], base=0, channel_multiplier=1)
-        clear(0, range(4))
-        nc.vector.tensor_scalar(out=ident[:], in0=apart[:], scalar1=0.0, scalar2=None, op0=EQUAL)
-        load_window(0, 0, 2)
-        load_window(0, 2, 4)
+        nc.vector.memset(dz[:].bitcast(F32)[:, 1:], 0.0)
+        load_window(0, 0)
+        load_window(0, 1)
         load_half("k", 0, 0)
         load_half("k", 0, 1)
-        load_window(1)
+        load_window(1, 0)
+        load_window(1, 1)
         load("k", 1)
         load("w", 0)
         load("w", 1)
@@ -262,55 +257,64 @@ def tile_localattention_pa_v_kernel(tc, x, Wq, bq, k, p, grad_out, out_0, out_1)
         load("x", 1)
         for h in range(2):
             row_sums(0, (2 * h, 2 * h + 1))
+            if h == 0:
+                nc.vector.tensor_scalar(out=ident[:], in0=apart[:], scalar1=0.0, scalar2=None, op0=EQUAL)
             soft(0, (2 * h, 2 * h + 1))
             empty(A, turn_dz(0, h))
-        clear(1, (0, 1))
-        weave("k", 0, 0)
-        clear(1, (2, 3))
-        weave("k", 0, 1, eng=A)
-        quant("k", 0, 0, 2)
-        quant_dz(0)
-        row_sums(1, range(4))
-        soft(1, range(4))
+        weave("k", 0, 0, 0, 256)
+        weave("k", 0, 0, 256, 512)
+        weave("k", 0, 1, 0, 320, eng=A)
+        quant("k", 0, 0, 1)
+        quant_dz(0, 0, 2)
+        quant("k", 0, 1, 2)
+        quant_dz(0, 2, 4)
+        weave("k", 0, 1, 320, 512)
+        row_sums(1, (0, 1))
         quant("k", 0, 2, 4)
-        for t in range(4):
+        row_sums(1, (2, 3))
+        soft(1, range(4))
+        empty(A, dh(0, 0, 0, 256))
+        for t in range(1, 4):
             empty(A, dh(0, t, 0))
+        empty(A, dh(0, 0, 1))
+        empty(A, dh(0, 1, 1))
         empty(A, turn_dz(1, 0), turn_dz(1, 1))
-        empty(A, dh(0, 0, 1), dh(0, 1, 1))
-        empty(A, dh(0, 2, 1), dh(0, 3, 1))
         weave("k", 1, 0)
         weave("k", 1, 1)
         quant("k", 1, 0, 2)
         quant_dz(1)
         quant("k", 1, 2, 4)
-        empty(A, turn_dq(0, 0), turn_dq(0, 1))
-        weave("w", 0, 0, 0, 192, A)
-        empty(A, turn_dq(0, 2), turn_dq(0, 3))
-        weave("w", 0, 0, 192, 512)
+        empty(A, dh(0, 2, 1))
+        empty(A, turn_dq(0, 0))
+        empty(A, dh(0, 3, 1))
+        empty(A, turn_dq(0, 1))
+        empty(A, turn_dq(0, 2))
+        empty(A, dh(1, 0, 0))
+        empty(A, dh(1, 0, 1))
+        empty(A, turn_dq(0, 3))
+        weave("w", 0, 0)
         weave("w", 0, 1)
         weave("w", 1, 0)
         quant_a(0, 2)
         quant("w", 0)
-        held = [dh(1, t, h) for t in range(4) for h in range(2)]
         weave("w", 1, 1)
+        quant("w", 1, 0, 2)
+        quant("w", 1, 2, 4)
         quant_a(2, 4)
-        quant("w", 1)
-        empty(A, *held[0:2])
+        for t in range(1, 4):
+            empty(A, dh(1, t, 0))
+            empty(A, dh(1, t, 1))
+            if t > 1:
+                empty(A, turn_dq(1, t - 2))
         first = [product("a", t, 0) for t in range(2)]
-        empty(A, *held[2:4])
-        turned = [turn_dq(1, t) for t in range(2)]
-        empty(A, *held[4:6])
-        second = [product("a", t, 1) for t in range(2)]
-        empty(A, *held[6:8])
         late = [turn_dq(1, t) for t in range(2, 4)]
-        empty(A, *turned)
-        empty(A, second[0], first[0])
-        store("a", 0)
-        empty(A, first[1], second[1])
-        store("a", 1)
-        third = [product("a", 2, h) for h in range(2)]
+        empty(A, first[0])
+        empty(A, first[1])
         empty(A, late[0])
-        empty(A, *third)
+        for t in range(2):
+            empty(A, product("a", t, 1))
+            store("a", t)
+        whole("a", 2, A, A)
         store("a", 2)
         empty(A, late[1])
         whole("a", 3)
@@ -319,20 +323,21 @@ def tile_localattention_pa_v_kernel(tc, x, Wq, bq, k, p, grad_out, out_0, out_1)
         weave("x", 1, 0)
         quant_a(4, 6)
         weave("x", 0, 1)
-        quant("x", 0)
-        weave("x", 1, 1)
         quant_a(6, 8)
         weave_dq(0)
-        quant("x", 1)
+        quant("x", 0)
+        weave("x", 1, 1)
         quant_b(0)
+        quant("x", 1, 0, 2)
+        weave_dq(1)
+        quant("x", 1, 2, 4)
         for t in range(4, 8):
             whole("a", t)
             store("a", t)
-        weave_dq(1)
         for s in range(1, 8):
+            quant_b(s)
             if s < 7:
                 weave_dq(s + 1)
-            quant_b(s)
         for s in range(8):
-            whole("b", s, A, V if s >= 4 else None)
+            whole("b", s, A, V if s >= 6 else A)
             store("b", s)

@@ -11,7 +11,7 @@ WIN_STEP = 122
 WIN_PAIR = 250
 WIN_PITCH = 160
 GRP_BUFS = 3
-RUN = 4
+RUN = 8
 ROOM = {"a": ("raw_k1", "raw_w0", "raw_w1", "room0"), "b": ("room1", "room2", "raw_x0", "raw_x1")}
 
 F32 = mybir.dt.float32
@@ -293,14 +293,14 @@ def tile_localattention_pa_v_kernel(tc, x, Wq, bq, k, p, grad_out, out_0, out_1)
         empty(A, dh(1, 0, 1))
         empty(A, turn_dq(0, 3))
         weave("w", 0, 0)
-        weave("w", 0, 1)
         weave("w", 1, 0)
         quant_a(0, 2)
         quant("w", 0)
+        weave("w", 0, 1)
+        quant_a(2, 4)
         weave("w", 1, 1)
         quant("w", 1, 0, 2)
         quant("w", 1, 2, 4)
-        quant_a(2, 4)
         for t in range(1, 4):
             empty(A, dh(1, t, 0))
             empty(A, dh(1, t, 1))
@@ -308,14 +308,11 @@ def tile_localattention_pa_v_kernel(tc, x, Wq, bq, k, p, grad_out, out_0, out_1)
                 empty(A, turn_dq(1, t - 2))
         first = [product("a", t, 0) for t in range(2)]
         late = [turn_dq(1, t) for t in range(2, 4)]
-        empty(A, first[0])
-        empty(A, first[1])
-        empty(A, late[0])
-        for t in range(2):
+        empty(A, *first)
+        empty(A, product("a", 2, 0), late[0])
+        for t in range(3):
             empty(A, product("a", t, 1))
             store("a", t)
-        whole("a", 2, A, A)
-        store("a", 2)
         empty(A, late[1])
         whole("a", 3)
         store("a", 3)

@@ -198,10 +198,11 @@ def tile_localattention_pa_v_kernel(tc, x, Wq, bq, k, p, grad_out, out_0, out_1)
             cols = slice(256 * t0, 256 * t1)
             nc.vector.quantize_mx(out=dqc["a"][g][:, cols].bitcast(E5M2), scales=dqs["a"][g][:, cols], in_=dq["a"][g][:, 1024 * t0 : 1024 * t1])
 
-        def weave_dq(s):
-            dqw[s] = keep.tile([P, 1024], BF16, name=f"dqw{s}", tag="dqw", bufs=4, align_bytes=64)
-            src = dqn[:].rearrange("p (b t s c i) -> p s b c t i", b=2, t=4, s=8, i=RUN)[:, s]
-            nc.vector.tensor_copy(out=dqw[s][:].rearrange("p (b c i t) -> p b c t i", b=2, i=RUN, t=4), in_=src)
+        def weave_dq(s, b0=0, b1=2):
+            if s not in dqw:
+                dqw[s] = keep.tile([P, 1024], BF16, name=f"dqw{s}", tag="dqw", bufs=4, align_bytes=64)
+            src = dqn[:].rearrange("p (b t s c i) -> p s b c t i", b=2, t=4, s=8, i=RUN)[:, s, b0:b1]
+            nc.vector.tensor_copy(out=dqw[s][:].rearrange("p (b c i t) -> p b c t i", b=2, i=RUN, t=4)[:, b0:b1], in_=src)
 
         def quant_b(s):
             cols = slice(256 * (s % 4), 256 * (s % 4 + 1))
@@ -320,8 +321,8 @@ def tile_localattention_pa_v_kernel(tc, x, Wq, bq, k, p, grad_out, out_0, out_1)
         weave("x", 1, 0)
         quant_a(4, 6)
         weave("x", 0, 1)
-        quant_a(6, 8)
         weave_dq(0)
+        quant_a(6, 8)
         quant("x", 0)
         weave("x", 1, 1)
         quant_b(0)
@@ -331,10 +332,13 @@ def tile_localattention_pa_v_kernel(tc, x, Wq, bq, k, p, grad_out, out_0, out_1)
         for t in range(4, 8):
             whole("a", t)
             store("a", t)
-        for s in range(1, 8):
-            quant_b(s)
+        quant_b(1)
+        weave_dq(2, 0, 1)
+        for s in range(2, 8):
+            weave_dq(s, 1, 2)
             if s < 7:
-                weave_dq(s + 1)
+                weave_dq(s + 1, 0, 1)
+            quant_b(s)
         for s in range(8):
-            whole("b", s, A, V if s >= 6 else A)
+            whole("b", s, A, V if s >= 5 else A)
             store("b", s)

from contextlib import ExitStack

import concourse.mybir as mybir

B, S, D, E = 2, 512, 1024, 1024
HALF = 5
T = B * S
P = 128
WIN = 140
WIN_STEP = 122
WIN_PAIR = 250
WIN_PITCH = 160
GRP_BUFS = 3
RUN = 8
ROOM = {"a": ("raw_k1", "raw_w0", "raw_w1", "room0"), "b": ("room1", "room2", "raw_x0", "raw_x1")}

F32 = mybir.dt.float32
BF16 = mybir.dt.bfloat16
U32 = mybir.dt.uint32
I32 = mybir.dt.int32
U8 = mybir.dt.uint8
E4M3 = mybir.dt.float8_e4m3fn_x4
E5M2 = mybir.dt.float8_e5m2_x4
MULT = mybir.AluOpType.mult
SUB = mybir.AluOpType.subtract
EQUAL = mybir.AluOpType.is_equal
COPY = mybir.ActivationFunctionType.Copy

FLOPS = 2 * B * S * S * E + 4 * T * E * D
BAND = B * (S * (2 * HALF + 1) - HALF * (HALF + 1))
BYTES = 2 * (T * D + E * D + T * E) + 6 * BAND + 4 * (T * D + E * D)


def tile_localattention_pa_v_kernel(tc, x, Wq, bq, k, p, grad_out, out_0, out_1):
    nc = tc.nc
    with ExitStack() as ctx:
        keep = ctx.enter_context(tc.tile_pool(name="keep", bufs=1))
        psum = ctx.enter_context(tc.psum_pool(name="psum", bufs=1))
        ctx.enter_context(tc.manual_schedule())

        def tiles(name, shape, dtype, n=2):
            return [keep.tile(shape, dtype, name=f"{name}{i}", tag=f"{name}{i}", align_bytes=64) for i in range(n)]

        ident = keep.tile([P, P], F32, name="ident", tag="ident", align_bytes=64)
        apart = keep.tile([P, P], I32, name="apart", tag="apart", align_bytes=64)
        pw = tiles("pw", [P, 4, WIN_PITCH], F32)
        gw = tiles("gw", [P, 4, WIN_PITCH], BF16)
        prod = keep.tile([P, 4, WIN_PITCH], F32, name="prod", tag="prod", align_bytes=64)
        rsum = tiles("rsum", [P, 4], F32)
        dz = keep.tile([P, 4 * S], BF16, name="dz", tag="dz", align_bytes=64)
        dzg = tiles("dzg", [P, 4 * S], BF16)
        dzc = tiles("dzc", [P, S], U32)
        dzs = tiles("dzs", [P, S], U8)
        raw, grp, res = {}, {}, {}
        code = {n: tiles(n + "code", [P, 1024], U32) for n in ("k", "w", "x")}
        scale = {n: tiles(n + "scale", [P, 1024], U8) for n in ("k", "w", "x")}
        dqn = keep.tile([P, 8192], BF16, name="dqn", tag="dqn", align_bytes=64)
        dq = {"a": tiles("dqa", [P, 4096], BF16)}
        dqw = {}
        dqc = {n: tiles("dqc" + n, [P, 1024], U32) for n in ("a", "b")}
        dqs = {n: tiles("dqs" + n, [P, 1024], U8) for n in ("a", "b")}

        def grouped(n, o):
            if (n, o) not in grp:
                grp[n, o] = keep.tile([P, 4096], BF16, name=f"grp_{n}{o}", tag="grp", bufs=GRP_BUFS, align_bytes=64)
            return grp[n, o]

        spare = list(range(8))

        def bank(dtype=F32, cols=512):
            n = spare[0]
            spare.remove(n)
            return n, psum.tile([P, cols], dtype, name=f"bank{n}", tag=f"bank{n}")

        V, A = "V", "A"

        def copy(eng, out, in_):
            if eng == V:
                nc.vector.tensor_copy(out=out, in_=in_)
            else:
                nc.scalar.copy(out=out, in_=in_)

        def empty(eng, *jobs):
            for n, job in reversed(jobs):
                job(eng)
            spare.extend(n for n, job in jobs)

        def load_window(b, h):
            step = P * S + WIN_STEP
            at = (b * S + 2 * P * h) * S + WIN_PAIR * h
            for dst, src in ((gw[b], grad_out), (pw[b], p)):
                flat = src.rearrange("b s j -> (b s j)")
                if h == 0:
                    rows = flat[at : at + 2 * step].rearrange("(i y) -> i y", i=2)[:, : P * S]
                    win = rows.rearrange("i (r j) -> r i j", j=S)[:, :, :WIN]
                else:
                    back = at - WIN_STEP - (S - WIN)
                    rows = flat[back : back + 2 * step].rearrange("(i y) -> i y", i=2)[:, WIN_STEP:]
                    win = rows.rearrange("i (r j) -> r i j", j=S)[:, :, S - WIN :]
                nc.sync.dma_start(out=dst[:, 2 * h : 2 * h + 2, :WIN], in_=win)

        def rows_of(n, b):
            return {"k": lambda: k[b], "x": lambda: x[b], "w": lambda: Wq[512 * b : 512 * (b + 1), :]}[n]().rearrange("(p j) c -> p j c", j=4)

        def load(n, b):
            t = keep.tile([P, 4, 1024], BF16, name=f"raw_{n}{b}", tag=f"raw_{n}{b}", align_bytes=64)
            nc.sync.dma_start(out=t[:], in_=rows_of(n, b))
            for h in range(2):
                raw[n, b, h] = t[:, :, 512 * h : 512 * (h + 1)]

        def load_half(n, b, h):
            t = keep.tile([P, 4, 512], BF16, name=f"raw_{n}{b}{h}", tag=f"raw_{n}{b}{h}", align_bytes=64)
            nc.sync.dma_start(out=t[:], in_=rows_of(n, b)[:, :, 512 * h : 512 * (h + 1)])
            raw[n, b, h] = t[:]

        def band(i):
            lo, hi = max(P * i - HALF - 1, 0), min(P * (i + 1) + HALF + 1, S)
            at = WIN_PAIR * (i // 2) + WIN_STEP * (i % 2)
            return slice(lo, hi), slice(lo - at, hi - at)

        def row_sums(b, tiles_):
            for i in tiles_:
                w = band(i)[1]
                nc.vector.scalar_tensor_tensor(out=prod[:, i, w], in0=gw[b][:, i, w], scalar=1.0, in1=pw[b][:, i, w], op0=MULT, op1=MULT, accum_out=rsum[b][:, i : i + 1])

        def soft(b, tiles_):
            for i in tiles_:
                cols, w = band(i)
                dst = dz[:].rearrange("p (i u m) -> p i u m", i=4, u=2)[:, i, :, cols.start // 2 : cols.stop // 2]
                g, q = (src[b][:, i, w].rearrange("p (m u) -> p u m", u=2) for src in (gw, pw))
                nc.vector.scalar_tensor_tensor(out=dst, in0=g, scalar=rsum[b][:, i : i + 1], in1=q, op0=SUB, op1=MULT)

        def turn_dz(b, h):
            n, t = bank()
            for i in range(2):
                words = dz[:, S * (2 * h + i) : S * (2 * h + i + 1)].bitcast(F32)
                for u in range(2):
                    at = 256 * u + 128 * i
                    nc.tensor.transpose(t[:, at : at + 128], words[:, P * u : P * (u + 1)], ident[:])
            words = dzg[b][:].bitcast(F32).rearrange("p (t m u) -> p t m u", t=4, u=2)
            return n, lambda eng: copy(eng, words[:, :, 64 * h : 64 * (h + 1), :], t[:].rearrange("p (u m t) -> p t m u", u=2, t=4))

        def quant_dz(b, t0=0, t1=4):
            cols = slice(P * t0, P * t1)
            nc.vector.quantize_mx(out=dzc[b][:, cols].bitcast(E5M2), scales=dzs[b][:, cols], in_=dzg[b][:, S * t0 : S * t1])

        def home(n, b, h):
            return (b, h) if n == "k" else (h, b)

        def woven(n, b, h):
            o, i = home(n, b, h)
            return grouped(n, o)[:, 2048 * i : 2048 * (i + 1)]

        def places(n, rows):
            j = "(u e)" if n == "x" else "(e u)"
            return rows.rearrange("p %s (c i) -> p c u e i" % j, u=2, i=RUN)

        def weave(n, b, h, c0=0, c1=512, eng=V):
            dst = woven(n, b, h)[:, 4 * c0 : 4 * c1].rearrange("p (c i u e) -> p c u e i", i=RUN, u=2, e=2)
            copy(eng, dst, places(n, raw[n, b, h][:, :, c0:c1]))

        def quant(n, o, c0=0, c1=4):
            cols = slice(256 * c0, 256 * c1)
            nc.vector.quantize_mx(out=code[n][o][:, cols].bitcast(E4M3), scales=scale[n][o][:, cols], in_=grouped(n, o)[:, 1024 * c0 : 1024 * c1])

        def dh(b, t, h, width=512):
            n, o = bank()
            rows = slice(P * t, P * (t + 1))
            for c in range(0, 512, width):
                cols = slice(512 * h + c, 512 * h + c + width)
                nc.tensor.matmul_mx(out=o[:, c : c + width], lhsT=dzc[b][:, rows].bitcast(E5M2), lhsT_scale=dzs[b][:, rows],
                                    rhs=code["k"][b][:, cols].bitcast(E4M3), rhs_scale=scale["k"][b][:, cols], start=True, stop=True)
            at = 4096 * b + 1024 * t + 512 * h

            dst = dqn[:, at : at + 512].rearrange("p (u m) -> p u m", u=2)
            src = o[:].rearrange("p (m u) -> p u m", u=2)

            def take(eng):
                if eng == A:
                    nc.scalar.activation(out=dst, in_=src, func=COPY, scale=1.0 / 32.0)
                else:
                    nc.vector.tensor_scalar(out=dst, in0=src, scalar1=1.0 / 32.0, scalar2=None, op0=MULT)

            return n, take

        def turn_dq(b, t):
            n, o = bank()
            words = dqn[:, 4096 * b + 1024 * t : 4096 * b + 1024 * (t + 1)].bitcast(F32)
            for g in range(2):
                for u in range(2):
                    at = 256 * g + 128 * u
                    nc.tensor.transpose(o[:, at : at + 128], words[:, at : at + 128], ident[:])
            dst = dq["a"][b][:, 1024 * t : 1024 * (t + 1)].bitcast(F32).rearrange("p (g m u) -> p g m u", g=2, u=2)
            return n, lambda eng: copy(eng, dst, o[:].rearrange("p (g u m) -> p g m u", g=2, u=2))

        def quant_a(i0, i1):
            g, t0, t1 = i0 // 4, i0 % 4, (i1 - 1) % 4 + 1
            cols = slice(256 * t0, 256 * t1)
            nc.vector.quantize_mx(out=dqc["a"][g][:, cols].bitcast(E5M2), scales=dqs["a"][g][:, cols], in_=dq["a"][g][:, 1024 * t0 : 1024 * t1])

        def weave_dq(s, b0=0, b1=2):
            if s not in dqw:
                dqw[s] = keep.tile([P, 1024], BF16, name=f"dqw{s}", tag="dqw", bufs=4, align_bytes=64)
            src = dqn[:].rearrange("p (b t s c i) -> p s b c t i", b=2, t=4, s=8, i=RUN)[:, s, b0:b1]
            nc.vector.tensor_copy(out=dqw[s][:].rearrange("p (b c i t) -> p b c t i", b=2, i=RUN, t=4)[:, b0:b1], in_=src)

        def quant_b(s):
            cols = slice(256 * (s % 4), 256 * (s % 4 + 1))
            nc.vector.quantize_mx(out=dqc["b"][s // 4][:, cols].bitcast(E5M2), scales=dqs["b"][s // 4][:, cols], in_=dqw[s][:])

        def still(n, i, g):
            at = 256 * (i % 4) + P * g
            return slice(at, at + P)

        def rows_out(n, i):
            if n == "a":
                return out_0[i // 4].rearrange("(m t) d -> m t d", t=4)[:, i % 4, :]
            return out_1.rearrange("(g q m u) d -> g u m q d", g=2, q=2, u=2)[i // 4, i // 2 % 2][:, i % 2, :]

        def product(n, i, h):
            other = {"a": "w", "b": "x"}[n]
            slot, o = bank()
            for g in range(2):
                mine = still(n, i, g)
                cols = slice(512 * g, 512 * (g + 1))
                nc.tensor.matmul_mx(out=o[:], lhsT=dqc[n][i // 4][:, mine].bitcast(E5M2), lhsT_scale=dqs[n][i // 4][:, mine],
                                    rhs=code[other][h][:, cols].bitcast(E4M3), rhs_scale=scale[other][h][:, cols], start=(g == 0), stop=(g == 1))

            def take(eng):
                if (n, i // 2) not in res:
                    res[n, i // 2] = keep.tile([P, 2, 1024], F32, name=f"res_{n}{i // 2}", tag=ROOM[n][i // 2], align_bytes=64)
                copy(eng, res[n, i // 2][:, i % 2, 512 * h : 512 * (h + 1)], o[:])

            return slot, take

        def whole(n, i, eng=A, other=None):
            if other is None:
                empty(eng, product(n, i, 0), product(n, i, 1))
            else:
                empty(eng, product(n, i, 0))
                empty(other, product(n, i, 1))

        def store(n, i):
            nc.sync.dma_start(out=rows_out(n, i), in_=res[n, i // 2][:, i % 2, :])

        nc.gpsimd.iota(apart[:], pattern=[[-1, P]], base=0, channel_multiplier=1)
        nc.vector.memset(dz[:].bitcast(F32)[:, 1:], 0.0)
        load_window(0, 0)
        load_window(0, 1)
        load_half("k", 0, 0)
        load_half("k", 0, 1)
        load_window(1, 0)
        load_window(1, 1)
        load("k", 1)
        load("w", 0)
        load("w", 1)
        load("x", 0)
        load("x", 1)
        for h in range(2):
            row_sums(0, (2 * h, 2 * h + 1))
            if h == 0:
                nc.vector.tensor_scalar(out=ident[:], in0=apart[:], scalar1=0.0, scalar2=None, op0=EQUAL)
            soft(0, (2 * h, 2 * h + 1))
            empty(A, turn_dz(0, h))
        weave("k", 0, 0, 0, 256)
        weave("k", 0, 0, 256, 512)
        weave("k", 0, 1, 0, 320, eng=A)
        quant("k", 0, 0, 1)
        quant_dz(0, 0, 2)
        quant("k", 0, 1, 2)
        quant_dz(0, 2, 4)
        weave("k", 0, 1, 320, 512)
        row_sums(1, (0, 1))
        quant("k", 0, 2, 4)
        row_sums(1, (2, 3))
        soft(1, range(4))
        empty(A, dh(0, 0, 0, 256))
        for t in range(1, 4):
            empty(A, dh(0, t, 0))
        empty(A, dh(0, 0, 1))
        empty(A, dh(0, 1, 1))
        empty(A, turn_dz(1, 0), turn_dz(1, 1))
        weave("k", 1, 0)
        weave("k", 1, 1)
        quant("k", 1, 0, 2)
        quant_dz(1)
        quant("k", 1, 2, 4)
        empty(A, dh(0, 2, 1))
        empty(A, turn_dq(0, 0))
        empty(A, dh(0, 3, 1))
        empty(A, turn_dq(0, 1))
        empty(A, turn_dq(0, 2))
        empty(A, dh(1, 0, 0))
        empty(A, dh(1, 0, 1))
        empty(A, turn_dq(0, 3))
        weave("w", 0, 0)
        weave("w", 1, 0)
        quant_a(0, 2)
        quant("w", 0)
        weave("w", 0, 1)
        quant_a(2, 4)
        weave("w", 1, 1)
        quant("w", 1, 0, 2)
        quant("w", 1, 2, 4)
        for t in range(1, 4):
            empty(A, dh(1, t, 0))
            empty(A, dh(1, t, 1))
            if t > 1:
                empty(A, turn_dq(1, t - 2))
        first = [product("a", t, 0) for t in range(2)]
        late = [turn_dq(1, t) for t in range(2, 4)]
        empty(A, *first)
        empty(A, product("a", 2, 0), late[0])
        for t in range(3):
            empty(A, product("a", t, 1))
            store("a", t)
        empty(A, late[1])
        whole("a", 3)
        store("a", 3)
        weave("x", 0, 0)
        weave("x", 1, 0)
        quant_a(4, 6)
        weave("x", 0, 1)
        weave_dq(0)
        quant_a(6, 8)
        quant("x", 0)
        weave("x", 1, 1)
        quant_b(0)
        quant("x", 1, 0, 2)
        weave_dq(1)
        quant("x", 1, 2, 4)
        for t in range(4, 8):
            whole("a", t)
            store("a", t)
        quant_b(1)
        weave_dq(2, 0, 1)
        for s in range(2, 8):
            weave_dq(s, 1, 2)
            if s < 7:
                weave_dq(s + 1, 0, 1)
            quant_b(s)
        for s in range(8):
            whole("b", s, A, V if s >= 5 else A)
            store("b", s)
